import numpy as np
import ml_dtypes


def mxq(x, axis, fmt="e4m3"):
    dtype, down = {"e4m3": (ml_dtypes.float8_e4m3fn, 7), "e5m2": (ml_dtypes.float8_e5m2, 14)}[fmt]
    v = np.moveaxis(np.asarray(x, np.float32).astype(ml_dtypes.bfloat16).astype(np.float64), axis, -1)
    blocks = v.reshape(v.shape[:-1] + (-1, 32))
    amax = np.abs(blocks).max(-1, keepdims=True)
    byte = np.maximum(np.where(amax > 0, np.frexp(amax)[1] - 1 + 127, 0) - down, 1)
    scale = np.exp2(byte - 127.0)
    codes = (blocks / scale).astype(np.float32).astype(dtype).astype(np.float64)
    return np.moveaxis((codes * scale).reshape(v.shape), -1, axis)


WIDE = False


def mx_kscale(k):
    if not WIDE:
        return np.ones(k)
    levels = np.array([10, -10, 5, -5, 0])
    a = np.random.permutation(np.resize(levels, k // 512 * 4)).reshape(k // 512, 4)
    idx = np.arange(k)
    return np.exp2(a[idx // 512, idx % 128 // 32])


BF16 = ml_dtypes.bfloat16


def bf(x):
    return np.asarray(x, np.float32).astype(BF16)


def f64(x):
    return np.asarray(x).astype(np.float64)


B, IN_CH, OUT_CH, KH, KW, H, W_IN = 4, 32, 512, 2, 2, 65, 65
HO, WO = H - KH + 1, W_IN - KW + 1
L = HO * WO
KD = KH * KW
F = IN_CH * KD * KD
MXB = 32


def setup_inputs():
    s = mx_kscale(F)[(np.arange(IN_CH) * KD * KD) // MXB * MXB]
    u = np.exp2(np.round(np.log2(s) / 2))
    return {"x": bf(np.random.standard_normal((B, IN_CH, H, W_IN)) * u[None, :, None, None]),
            "W": bf(np.random.standard_normal((OUT_CH, F)) / np.sqrt(F) / np.repeat(u * u, KD * KD)[None, :])}


def _unfold(x):
    patches = np.stack([x[:, :, i:i + HO, j:j + WO] for i in range(KH) for j in range(KW)], axis=2)
    return patches.reshape(B, IN_CH, KD, L).transpose(0, 3, 1, 2)


def reference(x, W):
    p = _unfold(f64(x))
    outer = np.einsum("blci,blcj->blcij", p, p)
    feat = outer.reshape(B, L, F)
    out = mxq(f64(W), 1, "e4m3") @ mxq(feat, 2, "e4m3").transpose(0, 2, 1)
    return out.reshape(B, OUT_CH, HO, WO)

@@ -1,0 +1,147 @@
+from contextlib import ExitStack
+
+import concourse.mybir as mybir
+from concourse.masks import make_identity
+
+BF16 = mybir.dt.bfloat16
+F32 = mybir.dt.float32
+U32 = mybir.dt.uint32
+U8 = mybir.dt.uint8
+FP8X4 = mybir.dt.float8_e4m3fn_x4
+MULT = mybir.AluOpType.mult
+
+P = 128
+B = 4
+C = 32
+SIDE = 65
+IMG = SIDE * SIDE
+GRID = 64
+L = GRID * GRID
+O = 512
+F = 512
+LEN = IMG - 1
+WIN = 512
+ROWS = WIN // GRID
+CHUNK = 2048
+DVE_ROWS = 5
+FLOPS = 2 * O * F * B * L
+
+
+def tile_fast2order_de_conv_t_kernel(tc, x, W, out):
+    nc = tc.nc
+    with ExitStack() as ctx:
+        const = ctx.enter_context(tc.tile_pool(name="const", bufs=1))
+        gpool = ctx.enter_context(tc.tile_pool(name="gpool", bufs=3))
+        cpool = ctx.enter_context(tc.tile_pool(name="cpool", bufs=3))
+        stage = ctx.enter_context(tc.tile_pool(name="stage", bufs=3))
+        psum = ctx.enter_context(tc.psum_pool(name="psum", bufs=6))
+        psum_x = ctx.enter_context(tc.psum_pool(name="psum_x", bufs=2))
+
+        w_sb = const.tile([P, 4, F], BF16, name="w_sb")
+        nc.scalar.dma_start(out=w_sb[:], in_=W.rearrange("(ob o) f -> o ob f", o=P))
+        xa = const.tile([P, B, IMG], BF16, name="xa")
+        xb = const.tile([P, B, IMG], BF16, name="xb")
+        xf = x.rearrange("n c h w -> n c (h w)")
+        for n in range(B):
+            for i0 in range(2):
+                for j0 in range(2):
+                    g0 = 2 * i0 + j0
+                    nc.sync.dma_start(out=xa[g0:P:4, n, 0:LEN], in_=xf[n, :, i0 : i0 + LEN])
+                    nc.sync.dma_start(out=xb[g0:P:4, n, 0:LEN], in_=xf[n, :, j0 : j0 + LEN])
+
+        ident = const.tile([P, P], BF16, name="ident")
+        make_identity(nc, ident[:])
+        w_perm = const.tile([P, 4, 4, P], BF16, name="w_perm")
+        wv = w_sb[:].rearrange(
+            "o ob (c i1 i0 j1 j0) -> o i1 j1 ob c i0 j0", c=C, i1=2, i0=2, j1=2, j0=2
+        )
+        for i1 in range(2):
+            for j1 in range(2):
+                nc.vector.tensor_copy(
+                    out=w_perm[:, :, 2 * i1 + j1, :].rearrange(
+                        "o ob (c i0 j0) -> o ob c i0 j0", c=C, i0=2, j0=2
+                    ),
+                    in_=wv[:, i1, j1],
+                )
+        wg = const.tile([P, O, 4], BF16, name="wg", align_bytes=64)
+        for ob in range(4):
+            xt = psum.tile([P, 4, P], BF16, name="xt", tag="bank")
+            for t in range(4):
+                nc.tensor.transpose(xt[:, t, :], w_perm[:, ob, t, :], ident[:])
+            nc.vector.tensor_copy(
+                out=wg[:, ob * P : (ob + 1) * P, :], in_=xt[:].rearrange("p t o -> p o t")
+            )
+        w_codes = const.tile([P, O], U32, name="w_codes", align_bytes=64)
+        w_scales = const.tile([P, O], U8, name="w_scales", align_bytes=64)
+        nc.vector.quantize_mx(
+            out=w_codes[:].bitcast(FP8X4),
+            scales=w_scales[:],
+            in_=wg[:].rearrange("p o t -> p (o t)"),
+        )
+
+        out_v = out.rearrange("n (mt o) y z -> n mt o (y z)", o=P)
+
+        chunks = []
+        for n in range(B):
+            if n < B - 1:
+                chunks.extend([(n, 0, 2048), (n, 2048, 2048)])
+            else:
+                chunks.extend([(n, 0, 2048), (n, 2048, 1024), (n, 3072, 512), (n, 3584, 512)])
+        for n, pos0, size in chunks:
+            st = stage.tile([P, 4, CHUNK], F32, name="st")
+            for wi in range(size // WIN):
+                y0 = (pos0 + wi * WIN) // GRID
+                xbp = psum_x.tile([P, ROWS, GRID], BF16, name="xbp")
+                nc.tensor.matmul(
+                    out=xbp[:],
+                    lhsT=ident[:],
+                    rhs=xb[:, n, SIDE * y0 : SIDE * (y0 + ROWS)].rearrange(
+                        "p (y r) -> p y r", y=ROWS
+                    )[:, :, 0:GRID],
+                    start=True,
+                    stop=True,
+                )
+                g = gpool.tile([P, WIN, 2, 2], BF16, name="g", align_bytes=64)
+                for r in range(ROWS):
+                    y = y0 + r
+                    a_rows = xa[:, n, SIDE * y : SIDE * (y + 2)].rearrange(
+                        "p (i r) -> p i r", i=2
+                    )[:, :, 0:GRID]
+                    in0 = a_rows.rearrange("p i z -> p z i").unsqueeze(3).to_broadcast([P, GRID, 2, 2])
+                    if r < DVE_ROWS:
+                        b_rows = xbp[:, r : r + 2, :]
+                        eng = nc.vector
+                    else:
+                        b_rows = xb[:, n, SIDE * y : SIDE * (y + 2)].rearrange(
+                            "p (j r) -> p j r", j=2
+                        )[:, :, 0:GRID]
+                        eng = nc.gpsimd
+                    eng.tensor_tensor(
+                        out=g[:, r * GRID : (r + 1) * GRID, :, :],
+                        in0=in0,
+                        in1=b_rows.rearrange("p j z -> p z j").unsqueeze(2).to_broadcast([P, GRID, 2, 2]),
+                        op=MULT,
+                    )
+                codes = cpool.tile([P, WIN], U32, name="codes", align_bytes=64)
+                scales = cpool.tile([P, WIN], U8, name="scales", align_bytes=64)
+                nc.vector.quantize_mx(
+                    out=codes[:].bitcast(FP8X4),
+                    scales=scales[:],
+                    in_=g[:].rearrange("p w i j -> p (w i j)"),
+                )
+                for mt in range(4):
+                    ps = psum.tile([P, WIN], F32, name="ps", tag="bank")
+                    nc.tensor.matmul_mx(
+                        out=ps[:],
+                        lhsT=w_codes[:, mt * P : (mt + 1) * P].bitcast(FP8X4),
+                        lhsT_scale=w_scales[:, mt * P : (mt + 1) * P],
+                        rhs=codes[:].bitcast(FP8X4),
+                        rhs_scale=scales[:],
+                        start=True,
+                        stop=True,
+                    )
+                    nc.scalar.copy(out=st[:, mt, wi * WIN : (wi + 1) * WIN], in_=ps[:])
+            for mt in range(4):
+                nc.sync.dma_start(
+                    out=out_v[n, mt][:, pos0 : pos0 + size], in_=st[:, mt, 0:size]
+                )

@@ -23,7 +23,7 @@ LEN = IMG - 1
 WIN = 512
 ROWS = WIN // GRID
 CHUNK = 2048
-DVE_ROWS = 5
+DVE_ROWS = 7
 FLOPS = 2 * O * F * B * L
 
 

@@ -19,11 +19,12 @@ GRID = 64
 L = GRID * GRID
 O = 512
 F = 512
-LEN = IMG - 1
-WIN = 512
-ROWS = WIN // GRID
-CHUNK = 2048
-DVE_ROWS = 7
+LEN = GRID * SIDE
+SLOT = 256
+WROWS = 7
+NG = 4
+PE_WINDOWS = 25
+STAGE = 35 * GRID
 FLOPS = 2 * O * F * B * L
 
 
@@ -31,7 +32,6 @@ def tile_fast2order_de_conv_t_kernel(tc, x, W, out):
     nc = tc.nc
     with ExitStack() as ctx:
         const = ctx.enter_context(tc.tile_pool(name="const", bufs=1))
-        gpool = ctx.enter_context(tc.tile_pool(name="gpool", bufs=3))
         cpool = ctx.enter_context(tc.tile_pool(name="cpool", bufs=3))
         stage = ctx.enter_context(tc.tile_pool(name="stage", bufs=3))
         psum = ctx.enter_context(tc.psum_pool(name="psum", bufs=6))
@@ -39,29 +39,35 @@ def tile_fast2order_de_conv_t_kernel(tc, x, W, out):
 
         w_sb = const.tile([P, 4, F], BF16, name="w_sb")
         nc.scalar.dma_start(out=w_sb[:], in_=W.rearrange("(ob o) f -> o ob f", o=P))
-        xa = const.tile([P, B, IMG], BF16, name="xa")
-        xb = const.tile([P, B, IMG], BF16, name="xb")
+        xa = const.tile([P, B, LEN], BF16, name="xa")
+        xb = const.tile([P, B, LEN], BF16, name="xb")
         xf = x.rearrange("n c h w -> n c (h w)")
         for n in range(B):
-            for i0 in range(2):
-                for j0 in range(2):
-                    g0 = 2 * i0 + j0
-                    nc.sync.dma_start(out=xa[g0:P:4, n, 0:LEN], in_=xf[n, :, i0 : i0 + LEN])
-                    nc.sync.dma_start(out=xb[g0:P:4, n, 0:LEN], in_=xf[n, :, j0 : j0 + LEN])
+            for i1 in range(2):
+                for j1 in range(2):
+                    g0 = 2 * i1 + j1
+                    nc.sync.dma_start(out=xa[g0:P:4, n, :], in_=xf[n, :, SIDE * i1 : SIDE * i1 + LEN])
+                    nc.sync.dma_start(out=xb[g0:P:4, n, :], in_=xf[n, :, SIDE * j1 : SIDE * j1 + LEN])
+
+        gs = []
+        for k in range(NG):
+            gt = const.tile([P, 2, SLOT, 4], BF16, name="g%d" % k, align_bytes=64)
+            nc.vector.memset(gt[:, :, 228:SLOT, :], 0.0)
+            gs.append(gt)
 
         ident = const.tile([P, P], BF16, name="ident")
         make_identity(nc, ident[:])
         w_perm = const.tile([P, 4, 4, P], BF16, name="w_perm")
         wv = w_sb[:].rearrange(
-            "o ob (c i1 i0 j1 j0) -> o i1 j1 ob c i0 j0", c=C, i1=2, i0=2, j1=2, j0=2
+            "o ob (c i1 i0 j1 j0) -> o i0 j0 ob c i1 j1", c=C, i1=2, i0=2, j1=2, j0=2
         )
-        for i1 in range(2):
-            for j1 in range(2):
+        for i0 in range(2):
+            for j0 in range(2):
                 nc.vector.tensor_copy(
-                    out=w_perm[:, :, 2 * i1 + j1, :].rearrange(
-                        "o ob (c i0 j0) -> o ob c i0 j0", c=C, i0=2, j0=2
+                    out=w_perm[:, :, 2 * i0 + j0, :].rearrange(
+                        "o ob (c i1 j1) -> o ob c i1 j1", c=C, i1=2, j1=2
                     ),
-                    in_=wv[:, i1, j1],
+                    in_=wv[:, i0, j0],
                 )
         wg = const.tile([P, O, 4], BF16, name="wg", align_bytes=64)
         for ob in range(4):
@@ -81,58 +87,82 @@ def tile_fast2order_de_conv_t_kernel(tc, x, W, out):
 
         out_v = out.rearrange("n (mt o) y z -> n mt o (y z)", o=P)
 
+        full = [(WROWS * w, WROWS) for w in range(9)]
+        last = (63, 1)
         chunks = []
         for n in range(B):
             if n < B - 1:
-                chunks.extend([(n, 0, 2048), (n, 2048, 2048)])
+                chunks.append((n, full[0:5]))
+                chunks.append((n, full[5:9] + [last]))
             else:
-                chunks.extend([(n, 0, 2048), (n, 2048, 1024), (n, 3072, 512), (n, 3584, 512)])
-        for n, pos0, size in chunks:
-            st = stage.tile([P, 4, CHUNK], F32, name="st")
-            for wi in range(size // WIN):
-                y0 = (pos0 + wi * WIN) // GRID
-                xbp = psum_x.tile([P, ROWS, GRID], BF16, name="xbp")
-                nc.tensor.matmul(
-                    out=xbp[:],
-                    lhsT=ident[:],
-                    rhs=xb[:, n, SIDE * y0 : SIDE * (y0 + ROWS)].rearrange(
-                        "p (y r) -> p y r", y=ROWS
-                    )[:, :, 0:GRID],
-                    start=True,
-                    stop=True,
-                )
-                g = gpool.tile([P, WIN, 2, 2], BF16, name="g", align_bytes=64)
-                for r in range(ROWS):
-                    y = y0 + r
-                    a_rows = xa[:, n, SIDE * y : SIDE * (y + 2)].rearrange(
-                        "p (i r) -> p i r", i=2
-                    )[:, :, 0:GRID]
-                    in0 = a_rows.rearrange("p i z -> p z i").unsqueeze(3).to_broadcast([P, GRID, 2, 2])
-                    if r < DVE_ROWS:
-                        b_rows = xbp[:, r : r + 2, :]
-                        eng = nc.vector
+                chunks.append((n, full[0:5]))
+                chunks.append((n, full[5:7]))
+                chunks.append((n, full[7:8]))
+                chunks.append((n, full[8:9] + [last]))
+
+        widx = 0
+        nfull = 0
+        for n, wins in chunks:
+            st = stage.tile([P, 4, STAGE], F32, name="st")
+            row_first = wins[0][0]
+            for y0, nrows in wins:
+                q0 = SIDE * y0
+                m = 228 if nrows == WROWS else 32
+                use_pe = False
+                if nrows == WROWS:
+                    use_pe = (nfull * PE_WINDOWS) % 36 < PE_WINDOWS
+                    nfull += 1
+                g = gs[widx % NG]
+                widx += 1
+                if use_pe:
+                    xad = psum_x.tile([P, 2 * SLOT, 2], BF16, name="xad")
+                    for h in range(2):
+                        nc.tensor.matmul(
+                            out=xad[:, h * SLOT : (h + 1) * SLOT, :],
+                            lhsT=ident[:],
+                            rhs=xa[:, n, q0 + h * SLOT : q0 + (h + 1) * SLOT]
+                            .unsqueeze(2)
+                            .to_broadcast([P, SLOT, 2]),
+                            start=True,
+                            stop=True,
+                        )
+                    xad_flat = xad[:].rearrange("p r e -> p (r e)")
+                for s in range(2):
+                    if use_pe:
+                        in0 = xad_flat[:, 2 * s : 2 * s + 4 * m].rearrange(
+                            "p (m i j) -> p m i j", i=2, j=2
+                        )
                     else:
-                        b_rows = xb[:, n, SIDE * y : SIDE * (y + 2)].rearrange(
-                            "p (j r) -> p j r", j=2
-                        )[:, :, 0:GRID]
-                        eng = nc.gpsimd
-                    eng.tensor_tensor(
-                        out=g[:, r * GRID : (r + 1) * GRID, :, :],
+                        in0 = (
+                            xa[:, n, q0 + s : q0 + s + 2 * m]
+                            .rearrange("p (m i) -> p m i", i=2)
+                            .unsqueeze(3)
+                            .to_broadcast([P, m, 2, 2])
+                        )
+                    in1 = (
+                        xb[:, n, q0 + s : q0 + s + 2 * m]
+                        .rearrange("p (m j) -> p m j", j=2)
+                        .unsqueeze(2)
+                        .to_broadcast([P, m, 2, 2])
+                    )
+                    nc.vector.tensor_tensor(
+                        out=g[:, s, 0:m, :].rearrange("p m (i j) -> p m i j", i=2),
                         in0=in0,
-                        in1=b_rows.rearrange("p j z -> p z j").unsqueeze(2).to_broadcast([P, GRID, 2, 2]),
+                        in1=in1,
                         op=MULT,
                     )
-                codes = cpool.tile([P, WIN], U32, name="codes", align_bytes=64)
-                scales = cpool.tile([P, WIN], U8, name="scales", align_bytes=64)
+                codes = cpool.tile([P, 2 * SLOT], U32, name="codes", align_bytes=64)
+                scales = cpool.tile([P, 2 * SLOT], U8, name="scales", align_bytes=64)
                 nc.vector.quantize_mx(
                     out=codes[:].bitcast(FP8X4),
                     scales=scales[:],
-                    in_=g[:].rearrange("p w i j -> p (w i j)"),
+                    in_=g[:].rearrange("p s m t -> p (s m t)"),
                 )
+                b0 = (y0 - row_first) * GRID
                 for mt in range(4):
-                    ps = psum.tile([P, WIN], F32, name="ps", tag="bank")
+                    ps = psum.tile([P, 2, SLOT], F32, name="ps", tag="bank")
                     nc.tensor.matmul_mx(
-                        out=ps[:],
+                        out=ps[:].rearrange("p s k -> p (s k)"),
                         lhsT=w_codes[:, mt * P : (mt + 1) * P].bitcast(FP8X4),
                         lhsT_scale=w_scales[:, mt * P : (mt + 1) * P],
                         rhs=codes[:].bitcast(FP8X4),
@@ -140,8 +170,33 @@ def tile_fast2order_de_conv_t_kernel(tc, x, W, out):
                         start=True,
                         stop=True,
                     )
-                    nc.scalar.copy(out=st[:, mt, wi * WIN : (wi + 1) * WIN], in_=ps[:])
+                    if nrows == WROWS:
+                        nc.scalar.copy(
+                            out=st[:, mt, b0 + 63 : b0 + 63 + 384]
+                            .rearrange("p (rho e) -> p rho e", e=128)[:, :, 0:66]
+                            .rearrange("p rho (k s) -> p rho k s", s=2),
+                            in_=ps[:, :, 32:227].rearrange("p s (rho k) -> p rho k s", k=65)[
+                                :, :, 0:33, :
+                            ],
+                        )
+                        nc.scalar.copy(
+                            out=st[:, mt, b0 : b0 + 384]
+                            .rearrange("p (rho e) -> p rho e", e=128)[:, :, 0:64]
+                            .rearrange("p rho (a s) -> p rho a s", s=2),
+                            in_=ps[:, :, 0:195].rearrange("p s (rho k) -> p rho k s", k=65)[
+                                :, :, 0:32, :
+                            ],
+                        )
+                        nc.scalar.copy(
+                            out=st[:, mt, b0 + 384 : b0 + 448].rearrange("p (a s) -> p a s", s=2),
+                            in_=ps[:, :, 195:227].rearrange("p s a -> p a s"),
+                        )
+                    else:
+                        nc.scalar.copy(
+                            out=st[:, mt, b0 : b0 + GRID].rearrange("p (a s) -> p a s", s=2),
+                            in_=ps[:, :, 0:32].rearrange("p s a -> p a s"),
+                        )
+            size = GRID * sum(w[1] for w in wins)
+            pos0 = GRID * row_first
             for mt in range(4):
-                nc.sync.dma_start(
-                    out=out_v[n, mt][:, pos0 : pos0 + size], in_=st[:, mt, 0:size]
-                )
+                nc.sync.dma_start(out=out_v[n, mt][:, pos0 : pos0 + size], in_=st[:, mt, 0:size])

@@ -38,16 +38,27 @@ def tile_fast2order_de_conv_t_kernel(tc, x, W, out):
         psum_x = ctx.enter_context(tc.psum_pool(name="psum_x", bufs=2))
 
         w_sb = const.tile([P, 4, F], BF16, name="w_sb")
-        nc.scalar.dma_start(out=w_sb[:], in_=W.rearrange("(ob o) f -> o ob f", o=P))
-        xa = const.tile([P, B, LEN], BF16, name="xa")
-        xb = const.tile([P, B, LEN], BF16, name="xb")
+        nc.sync.dma_start(out=w_sb[:], in_=W.rearrange("(ob o) f -> o ob f", o=P))
         xf = x.rearrange("n c h w -> n c (h w)")
+        xas = []
+        xbs = []
         for n in range(B):
-            for i1 in range(2):
-                for j1 in range(2):
-                    g0 = 2 * i1 + j1
-                    nc.sync.dma_start(out=xa[g0:P:4, n, :], in_=xf[n, :, SIDE * i1 : SIDE * i1 + LEN])
-                    nc.sync.dma_start(out=xb[g0:P:4, n, :], in_=xf[n, :, SIDE * j1 : SIDE * j1 + LEN])
+            xa_n = const.tile([P, LEN], BF16, name="xa%d" % n)
+            xb_n = const.tile([P, LEN], BF16, name="xb%d" % n)
+            xas.append(xa_n)
+            xbs.append(xb_n)
+            for c0, c1 in ((8, 24), (0, 8), (24, 32)):
+                for i1 in range(2):
+                    for j1 in range(2):
+                        g0 = 2 * i1 + j1
+                        nc.sync.dma_start(
+                            out=xa_n[g0 + 4 * c0 : 4 * c1 : 4, :],
+                            in_=xf[n, c0:c1, SIDE * i1 : SIDE * i1 + LEN],
+                        )
+                        nc.sync.dma_start(
+                            out=xb_n[g0 + 4 * c0 : 4 * c1 : 4, :],
+                            in_=xf[n, c0:c1, SIDE * j1 : SIDE * j1 + LEN],
+                        )
 
         gs = []
         for k in range(NG):
@@ -120,7 +131,7 @@ def tile_fast2order_de_conv_t_kernel(tc, x, W, out):
                         nc.tensor.matmul(
                             out=xad[:, h * SLOT : (h + 1) * SLOT, :],
                             lhsT=ident[:],
-                            rhs=xa[:, n, q0 + h * SLOT : q0 + (h + 1) * SLOT]
+                            rhs=xas[n][:, q0 + h * SLOT : q0 + (h + 1) * SLOT]
                             .unsqueeze(2)
                             .to_broadcast([P, SLOT, 2]),
                             start=True,
@@ -134,13 +145,13 @@ def tile_fast2order_de_conv_t_kernel(tc, x, W, out):
                         )
                     else:
                         in0 = (
-                            xa[:, n, q0 + s : q0 + s + 2 * m]
+                            xas[n][:, q0 + s : q0 + s + 2 * m]
                             .rearrange("p (m i) -> p m i", i=2)
                             .unsqueeze(3)
                             .to_broadcast([P, m, 2, 2])
                         )
                     in1 = (
-                        xb[:, n, q0 + s : q0 + s + 2 * m]
+                        xbs[n][:, q0 + s : q0 + s + 2 * m]
                         .rearrange("p (m j) -> p m j", j=2)
                         .unsqueeze(2)
                         .to_broadcast([P, m, 2, 2])
@@ -199,4 +210,4 @@ def tile_fast2order_de_conv_t_kernel(tc, x, W, out):
             size = GRID * sum(w[1] for w in wins)
             pos0 = GRID * row_first
             for mt in range(4):
-                nc.sync.dma_start(out=out_v[n, mt][:, pos0 : pos0 + size], in_=st[:, mt, 0:size])
+                nc.scalar.dma_start(out=out_v[n, mt][:, pos0 : pos0 + size], in_=st[:, mt, 0:size])

@@ -24,7 +24,7 @@ SLOT = 256
 WROWS = 7
 NG = 4
 PE_WINDOWS = 25
-STAGE = 35 * GRID
+STAGE = 22 * GRID
 FLOPS = 2 * O * F * B * L
 
 
@@ -33,7 +33,7 @@ def tile_fast2order_de_conv_t_kernel(tc, x, W, out):
     with ExitStack() as ctx:
         const = ctx.enter_context(tc.tile_pool(name="const", bufs=1))
         cpool = ctx.enter_context(tc.tile_pool(name="cpool", bufs=3))
-        stage = ctx.enter_context(tc.tile_pool(name="stage", bufs=3))
+        stage = ctx.enter_context(tc.tile_pool(name="stage", bufs=5))
         psum = ctx.enter_context(tc.psum_pool(name="psum", bufs=6))
         psum_x = ctx.enter_context(tc.psum_pool(name="psum_x", bufs=2))
 
@@ -47,18 +47,11 @@ def tile_fast2order_de_conv_t_kernel(tc, x, W, out):
             xb_n = const.tile([P, LEN], BF16, name="xb%d" % n)
             xas.append(xa_n)
             xbs.append(xb_n)
-            for c0, c1 in ((8, 24), (0, 8), (24, 32)):
-                for i1 in range(2):
-                    for j1 in range(2):
-                        g0 = 2 * i1 + j1
-                        nc.sync.dma_start(
-                            out=xa_n[g0 + 4 * c0 : 4 * c1 : 4, :],
-                            in_=xf[n, c0:c1, SIDE * i1 : SIDE * i1 + LEN],
-                        )
-                        nc.sync.dma_start(
-                            out=xb_n[g0 + 4 * c0 : 4 * c1 : 4, :],
-                            in_=xf[n, c0:c1, SIDE * j1 : SIDE * j1 + LEN],
-                        )
+            for i1 in range(2):
+                for j1 in range(2):
+                    g0 = 2 * i1 + j1
+                    nc.sync.dma_start(out=xa_n[g0:P:4, :], in_=xf[n, :, SIDE * i1 : SIDE * i1 + LEN])
+                    nc.sync.dma_start(out=xb_n[g0:P:4, :], in_=xf[n, :, SIDE * j1 : SIDE * j1 + LEN])
 
         gs = []
         for k in range(NG):
@@ -102,13 +95,16 @@ def tile_fast2order_de_conv_t_kernel(tc, x, W, out):
         last = (63, 1)
         chunks = []
         for n in range(B):
-            if n < B - 1:
-                chunks.append((n, full[0:5]))
-                chunks.append((n, full[5:9] + [last]))
+            if n == 0:
+                chunks.append((n, full[0:1]))
+                chunks.append((n, full[1:3]))
             else:
-                chunks.append((n, full[0:5]))
-                chunks.append((n, full[5:7]))
-                chunks.append((n, full[7:8]))
+                chunks.append((n, full[0:3]))
+            chunks.append((n, full[3:6]))
+            if n < B - 1:
+                chunks.append((n, full[6:9] + [last]))
+            else:
+                chunks.append((n, full[6:8]))
                 chunks.append((n, full[8:9] + [last]))
 
         widx = 0
@@ -210,4 +206,4 @@ def tile_fast2order_de_conv_t_kernel(tc, x, W, out):
             size = GRID * sum(w[1] for w in wins)
             pos0 = GRID * row_first
             for mt in range(4):
-                nc.scalar.dma_start(out=out_v[n, mt][:, pos0 : pos0 + size], in_=st[:, mt, 0:size])
+                nc.sync.dma_start(out=out_v[n, mt][:, pos0 : pos0 + size], in_=st[:, mt, 0:size])

@@ -37,6 +37,9 @@ def tile_fast2order_de_conv_t_kernel(tc, x, W, out):
         psum = ctx.enter_context(tc.psum_pool(name="psum", bufs=6))
         psum_x = ctx.enter_context(tc.psum_pool(name="psum_x", bufs=2))
 
+        ident = const.tile([P, P], BF16, name="ident")
+        make_identity(nc, ident[:])
+
         w_sb = const.tile([P, 4, F], BF16, name="w_sb")
         nc.sync.dma_start(out=w_sb[:], in_=W.rearrange("(ob o) f -> o ob f", o=P))
         xf = x.rearrange("n c h w -> n c (h w)")
@@ -50,8 +53,9 @@ def tile_fast2order_de_conv_t_kernel(tc, x, W, out):
             for i1 in range(2):
                 for j1 in range(2):
                     g0 = 2 * i1 + j1
-                    nc.sync.dma_start(out=xa_n[g0:P:4, :], in_=xf[n, :, SIDE * i1 : SIDE * i1 + LEN])
-                    nc.sync.dma_start(out=xb_n[g0:P:4, :], in_=xf[n, :, SIDE * j1 : SIDE * j1 + LEN])
+                    queue = nc.sync if n == 0 else nc.gpsimd
+                    queue.dma_start(out=xa_n[g0:P:4, :], in_=xf[n, :, SIDE * i1 : SIDE * i1 + LEN])
+                    queue.dma_start(out=xb_n[g0:P:4, :], in_=xf[n, :, SIDE * j1 : SIDE * j1 + LEN])
 
         gs = []
         for k in range(NG):
@@ -59,8 +63,6 @@ def tile_fast2order_de_conv_t_kernel(tc, x, W, out):
             nc.vector.memset(gt[:, :, 228:SLOT, :], 0.0)
             gs.append(gt)
 
-        ident = const.tile([P, P], BF16, name="ident")
-        make_identity(nc, ident[:])
         w_perm = const.tile([P, 4, 4, P], BF16, name="w_perm")
         wv = w_sb[:].rearrange(
             "o ob (c i1 i0 j1 j0) -> o i0 j0 ob c i1 j1", c=C, i1=2, i0=2, j1=2, j0=2

@@ -23,6 +23,8 @@ LEN = GRID * SIDE
 SLOT = 256
 WROWS = 7
 NG = 4
+NGP = 3
+GP_WINDOWS = (18, 20, 23, 25, 28, 30, 33)
 PE_WINDOWS = 25
 STAGE = 22 * GRID
 FLOPS = 2 * O * F * B * L
@@ -33,7 +35,7 @@ def tile_fast2order_de_conv_t_kernel(tc, x, W, out):
     with ExitStack() as ctx:
         const = ctx.enter_context(tc.tile_pool(name="const", bufs=1))
         cpool = ctx.enter_context(tc.tile_pool(name="cpool", bufs=3))
-        stage = ctx.enter_context(tc.tile_pool(name="stage", bufs=5))
+        stage = ctx.enter_context(tc.tile_pool(name="stage", bufs=4))
         psum = ctx.enter_context(tc.psum_pool(name="psum", bufs=6))
         psum_x = ctx.enter_context(tc.psum_pool(name="psum_x", bufs=2))
 
@@ -58,10 +60,14 @@ def tile_fast2order_de_conv_t_kernel(tc, x, W, out):
                     queue.dma_start(out=xb_n[g0:P:4, :], in_=xf[n, :, SIDE * j1 : SIDE * j1 + LEN])
 
         gs = []
-        for k in range(NG):
+        for k in range(NG + NGP):
             gt = const.tile([P, 2, SLOT, 4], BF16, name="g%d" % k, align_bytes=64)
             nc.vector.memset(gt[:, :, 228:SLOT, :], 0.0)
             gs.append(gt)
+        gsmall = []
+        for k in range(2):
+            gt = const.tile([P, GRID, 4], BF16, name="gsmall%d" % k, align_bytes=64)
+            gsmall.append(gt)
 
         w_perm = const.tile([P, 4, 4, P], BF16, name="w_perm")
         wv = w_sb[:].rearrange(
@@ -80,9 +86,14 @@ def tile_fast2order_de_conv_t_kernel(tc, x, W, out):
             xt = psum.tile([P, 4, P], BF16, name="xt", tag="bank")
             for t in range(4):
                 nc.tensor.transpose(xt[:, t, :], w_perm[:, ob, t, :], ident[:])
-            nc.vector.tensor_copy(
-                out=wg[:, ob * P : (ob + 1) * P, :], in_=xt[:].rearrange("p t o -> p o t")
-            )
+            if ob % 2 == 0:
+                nc.vector.tensor_copy(
+                    out=wg[:, ob * P : (ob + 1) * P, :], in_=xt[:].rearrange("p t o -> p o t")
+                )
+            else:
+                nc.scalar.copy(
+                    out=wg[:, ob * P : (ob + 1) * P, :], in_=xt[:].rearrange("p t o -> p o t")
+                )
         w_codes = const.tile([P, O], U32, name="w_codes", align_bytes=64)
         w_scales = const.tile([P, O], U8, name="w_scales", align_bytes=64)
         nc.vector.quantize_mx(
@@ -109,103 +120,154 @@ def tile_fast2order_de_conv_t_kernel(tc, x, W, out):
                 chunks.append((n, full[6:8]))
                 chunks.append((n, full[8:9] + [last]))
 
-        widx = 0
+        plan = []
+        gp_wins = []
         nfull = 0
+        ndve = 0
         for n, wins in chunks:
-            st = stage.tile([P, 4, STAGE], F32, name="st")
-            row_first = wins[0][0]
-            for y0, nrows in wins:
-                q0 = SIDE * y0
-                m = 228 if nrows == WROWS else 32
-                use_pe = False
+            for k, (y0, nrows) in enumerate(wins):
+                win = {
+                    "n": n,
+                    "y0": y0,
+                    "kind": "small",
+                    "pe": False,
+                    "slot": n % 2,
+                    "first": k == 0,
+                    "last": k == len(wins) - 1,
+                    "row_first": wins[0][0],
+                    "rows": sum(w[1] for w in wins),
+                }
                 if nrows == WROWS:
-                    use_pe = (nfull * PE_WINDOWS) % 36 < PE_WINDOWS
-                    nfull += 1
-                g = gs[widx % NG]
-                widx += 1
-                if use_pe:
-                    xad = psum_x.tile([P, 2 * SLOT, 2], BF16, name="xad")
-                    for h in range(2):
-                        nc.tensor.matmul(
-                            out=xad[:, h * SLOT : (h + 1) * SLOT, :],
-                            lhsT=ident[:],
-                            rhs=xas[n][:, q0 + h * SLOT : q0 + (h + 1) * SLOT]
-                            .unsqueeze(2)
-                            .to_broadcast([P, SLOT, 2]),
-                            start=True,
-                            stop=True,
-                        )
-                    xad_flat = xad[:].rearrange("p r e -> p (r e)")
-                for s in range(2):
-                    if use_pe:
-                        in0 = xad_flat[:, 2 * s : 2 * s + 4 * m].rearrange(
-                            "p (m i j) -> p m i j", i=2, j=2
-                        )
+                    if nfull in GP_WINDOWS:
+                        win["kind"] = "gp"
+                        win["slot"] = NG + len(gp_wins) % NGP
+                        win["order"] = len(gp_wins)
+                        gp_wins.append(win)
                     else:
-                        in0 = (
-                            xas[n][:, q0 + s : q0 + s + 2 * m]
-                            .rearrange("p (m i) -> p m i", i=2)
-                            .unsqueeze(3)
-                            .to_broadcast([P, m, 2, 2])
-                        )
-                    in1 = (
-                        xbs[n][:, q0 + s : q0 + s + 2 * m]
-                        .rearrange("p (m j) -> p m j", j=2)
+                        win["kind"] = "dve"
+                        win["slot"] = ndve % NG
+                        win["pe"] = (ndve * PE_WINDOWS) % (36 - len(GP_WINDOWS)) < PE_WINDOWS
+                        ndve += 1
+                    nfull += 1
+                plan.append(win)
+
+        state = {}
+
+        def emit_products(win):
+            n = win["n"]
+            q0 = SIDE * win["y0"]
+            small = win["kind"] == "small"
+            m = 32 if small else 228
+            gt = gsmall[win["slot"]] if small else gs[win["slot"]]
+            eng = nc.gpsimd if win["kind"] == "gp" else nc.vector
+            xad_flat = None
+            if win["pe"]:
+                xad = psum_x.tile([P, 2 * SLOT, 2], BF16, name="xad")
+                for h in range(2):
+                    nc.tensor.matmul(
+                        out=xad[:, h * SLOT : (h + 1) * SLOT, :],
+                        lhsT=ident[:],
+                        rhs=xas[n][:, q0 + h * SLOT : q0 + (h + 1) * SLOT]
                         .unsqueeze(2)
-                        .to_broadcast([P, m, 2, 2])
-                    )
-                    nc.vector.tensor_tensor(
-                        out=g[:, s, 0:m, :].rearrange("p m (i j) -> p m i j", i=2),
-                        in0=in0,
-                        in1=in1,
-                        op=MULT,
-                    )
-                codes = cpool.tile([P, 2 * SLOT], U32, name="codes", align_bytes=64)
-                scales = cpool.tile([P, 2 * SLOT], U8, name="scales", align_bytes=64)
-                nc.vector.quantize_mx(
-                    out=codes[:].bitcast(FP8X4),
-                    scales=scales[:],
-                    in_=g[:].rearrange("p s m t -> p (s m t)"),
-                )
-                b0 = (y0 - row_first) * GRID
-                for mt in range(4):
-                    ps = psum.tile([P, 2, SLOT], F32, name="ps", tag="bank")
-                    nc.tensor.matmul_mx(
-                        out=ps[:].rearrange("p s k -> p (s k)"),
-                        lhsT=w_codes[:, mt * P : (mt + 1) * P].bitcast(FP8X4),
-                        lhsT_scale=w_scales[:, mt * P : (mt + 1) * P],
-                        rhs=codes[:].bitcast(FP8X4),
-                        rhs_scale=scales[:],
+                        .to_broadcast([P, SLOT, 2]),
                         start=True,
                         stop=True,
                     )
-                    if nrows == WROWS:
-                        nc.scalar.copy(
-                            out=st[:, mt, b0 + 63 : b0 + 63 + 384]
-                            .rearrange("p (rho e) -> p rho e", e=128)[:, :, 0:66]
-                            .rearrange("p rho (k s) -> p rho k s", s=2),
-                            in_=ps[:, :, 32:227].rearrange("p s (rho k) -> p rho k s", k=65)[
-                                :, :, 0:33, :
-                            ],
-                        )
-                        nc.scalar.copy(
-                            out=st[:, mt, b0 : b0 + 384]
-                            .rearrange("p (rho e) -> p rho e", e=128)[:, :, 0:64]
-                            .rearrange("p rho (a s) -> p rho a s", s=2),
-                            in_=ps[:, :, 0:195].rearrange("p s (rho k) -> p rho k s", k=65)[
-                                :, :, 0:32, :
-                            ],
-                        )
-                        nc.scalar.copy(
-                            out=st[:, mt, b0 + 384 : b0 + 448].rearrange("p (a s) -> p a s", s=2),
-                            in_=ps[:, :, 195:227].rearrange("p s a -> p a s"),
-                        )
-                    else:
-                        nc.scalar.copy(
-                            out=st[:, mt, b0 : b0 + GRID].rearrange("p (a s) -> p a s", s=2),
-                            in_=ps[:, :, 0:32].rearrange("p s a -> p a s"),
-                        )
-            size = GRID * sum(w[1] for w in wins)
-            pos0 = GRID * row_first
+                xad_flat = xad[:].rearrange("p r e -> p (r e)")
+            for s in range(2):
+                if win["pe"]:
+                    in0 = xad_flat[:, 2 * s : 2 * s + 4 * m].rearrange(
+                        "p (m i j) -> p m i j", i=2, j=2
+                    )
+                else:
+                    in0 = (
+                        xas[n][:, q0 + s : q0 + s + 2 * m]
+                        .rearrange("p (m i) -> p m i", i=2)
+                        .unsqueeze(3)
+                        .to_broadcast([P, m, 2, 2])
+                    )
+                in1 = (
+                    xbs[n][:, q0 + s : q0 + s + 2 * m]
+                    .rearrange("p (m j) -> p m j", j=2)
+                    .unsqueeze(2)
+                    .to_broadcast([P, m, 2, 2])
+                )
+                dst = gt[:, s * m : (s + 1) * m, :] if small else gt[:, s, 0:m, :]
+                eng.tensor_tensor(
+                    out=dst.rearrange("p m (i j) -> p m i j", i=2), in0=in0, in1=in1, op=MULT
+                )
+
+        def emit_rest(win):
+            n = win["n"]
+            small = win["kind"] == "small"
+            width = GRID if small else 2 * SLOT
+            if small:
+                g_flat = gsmall[win["slot"]][:].rearrange("p m t -> p (m t)")
+                codes = cpool.tile([P, GRID], U32, name="codes_s", align_bytes=64)
+                scales = cpool.tile([P, GRID], U8, name="scales_s", align_bytes=64)
+            else:
+                g_flat = gs[win["slot"]][:].rearrange("p s m t -> p (s m t)")
+                codes = cpool.tile([P, 2 * SLOT], U32, name="codes", align_bytes=64)
+                scales = cpool.tile([P, 2 * SLOT], U8, name="scales", align_bytes=64)
+            nc.vector.quantize_mx(out=codes[:].bitcast(FP8X4), scales=scales[:], in_=g_flat)
+            if win["first"]:
+                state["st"] = stage.tile([P, 4, STAGE], F32, name="st")
+            st = state["st"]
+            b0 = (win["y0"] - win["row_first"]) * GRID
             for mt in range(4):
-                nc.sync.dma_start(out=out_v[n, mt][:, pos0 : pos0 + size], in_=st[:, mt, 0:size])
+                ps = psum.tile([P, 2, width // 2], F32, name="ps", tag="bank")
+                nc.tensor.matmul_mx(
+                    out=ps[:].rearrange("p s k -> p (s k)"),
+                    lhsT=w_codes[:, mt * P : (mt + 1) * P].bitcast(FP8X4),
+                    lhsT_scale=w_scales[:, mt * P : (mt + 1) * P],
+                    rhs=codes[:].bitcast(FP8X4),
+                    rhs_scale=scales[:],
+                    start=True,
+                    stop=True,
+                )
+                if small:
+                    nc.scalar.copy(
+                        out=st[:, mt, b0 : b0 + GRID].rearrange("p (a s) -> p a s", s=2),
+                        in_=ps[:].rearrange("p s a -> p a s"),
+                    )
+                else:
+                    nc.scalar.copy(
+                        out=st[:, mt, b0 + 63 : b0 + 63 + 384]
+                        .rearrange("p (rho e) -> p rho e", e=128)[:, :, 0:66]
+                        .rearrange("p rho (k s) -> p rho k s", s=2),
+                        in_=ps[:, :, 32:227].rearrange("p s (rho k) -> p rho k s", k=65)[
+                            :, :, 0:33, :
+                        ],
+                    )
+                    nc.scalar.copy(
+                        out=st[:, mt, b0 : b0 + 384]
+                        .rearrange("p (rho e) -> p rho e", e=128)[:, :, 0:64]
+                        .rearrange("p rho (a s) -> p rho a s", s=2),
+                        in_=ps[:, :, 0:195].rearrange("p s (rho k) -> p rho k s", k=65)[
+                            :, :, 0:32, :
+                        ],
+                    )
+                    nc.scalar.copy(
+                        out=st[:, mt, b0 + 384 : b0 + 448].rearrange("p (a s) -> p a s", s=2),
+                        in_=ps[:, :, 195:227].rearrange("p s a -> p a s"),
+                    )
+            if win["last"]:
+                size = GRID * win["rows"]
+                pos0 = GRID * win["row_first"]
+                for mt in range(4):
+                    nc.sync.dma_start(
+                        out=out_v[n, mt][:, pos0 : pos0 + size], in_=st[:, mt, 0:size]
+                    )
+            if win["kind"] == "gp" and win["order"] + NGP < len(gp_wins):
+                emit_products(gp_wins[win["order"] + NGP])
+
+        for win in gp_wins[0:NGP]:
+            emit_products(win)
+        prev = None
+        for win in plan:
+            if win["kind"] != "gp":
+                emit_products(win)
+            if prev is not None:
+                emit_rest(prev)
+            prev = win
+        emit_rest(prev)

@@ -23,9 +23,9 @@ LEN = GRID * SIDE
 SLOT = 256
 WROWS = 7
 NG = 4
-NGP = 3
-GP_WINDOWS = (18, 20, 23, 25, 28, 30, 33)
-PE_WINDOWS = 25
+NGP = 0
+GP_WINDOWS = ()
+PE_WINDOWS = 28
 STAGE = 22 * GRID
 FLOPS = 2 * O * F * B * L
 
@@ -35,7 +35,7 @@ def tile_fast2order_de_conv_t_kernel(tc, x, W, out):
     with ExitStack() as ctx:
         const = ctx.enter_context(tc.tile_pool(name="const", bufs=1))
         cpool = ctx.enter_context(tc.tile_pool(name="cpool", bufs=3))
-        stage = ctx.enter_context(tc.tile_pool(name="stage", bufs=4))
+        stage = ctx.enter_context(tc.tile_pool(name="stage", bufs=5))
         psum = ctx.enter_context(tc.psum_pool(name="psum", bufs=6))
         psum_x = ctx.enter_context(tc.psum_pool(name="psum_x", bufs=2))
 
@@ -163,13 +163,11 @@ def tile_fast2order_de_conv_t_kernel(tc, x, W, out):
             xad_flat = None
             if win["pe"]:
                 xad = psum_x.tile([P, 2 * SLOT, 2], BF16, name="xad")
-                for h in range(2):
+                for r0, r1 in ((0, SLOT), (SLOT, 2 * m + 1)):
                     nc.tensor.matmul(
-                        out=xad[:, h * SLOT : (h + 1) * SLOT, :],
+                        out=xad[:, r0:r1, :],
                         lhsT=ident[:],
-                        rhs=xas[n][:, q0 + h * SLOT : q0 + (h + 1) * SLOT]
-                        .unsqueeze(2)
-                        .to_broadcast([P, SLOT, 2]),
+                        rhs=xas[n][:, q0 + r0 : q0 + r1].unsqueeze(2).to_broadcast([P, r1 - r0, 2]),
                         start=True,
                         stop=True,
                     )

@@ -25,7 +25,8 @@ WROWS = 7
 NG = 4
 NGP = 0
 GP_WINDOWS = ()
-PE_WINDOWS = 28
+PLAIN_WINDOWS = (3, 7)
+XAW = 464
 STAGE = 22 * GRID
 FLOPS = 2 * O * F * B * L
 
@@ -41,23 +42,35 @@ def tile_fast2order_de_conv_t_kernel(tc, x, W, out):
 
         ident = const.tile([P, P], BF16, name="ident")
         make_identity(nc, ident[:])
+        swap = const.tile([P, P], BF16, name="swap")
+        nc.vector.tensor_copy(
+            out=swap[:].rearrange("p (c a b) -> p c a b", c=C, a=2, b=2),
+            in_=ident[:].rearrange("p (c b a) -> p c a b", c=C, a=2, b=2),
+        )
 
         w_sb = const.tile([P, 4, F], BF16, name="w_sb")
         nc.sync.dma_start(out=w_sb[:], in_=W.rearrange("(ob o) f -> o ob f", o=P))
         xf = x.rearrange("n c h w -> n c (h w)")
-        xas = []
         xbs = []
+        xa_part = const.tile([P, B, len(PLAIN_WINDOWS), XAW], BF16, name="xa_part")
         for n in range(B):
-            xa_n = const.tile([P, LEN], BF16, name="xa%d" % n)
             xb_n = const.tile([P, LEN], BF16, name="xb%d" % n)
-            xas.append(xa_n)
             xbs.append(xb_n)
             for i1 in range(2):
                 for j1 in range(2):
                     g0 = 2 * i1 + j1
                     queue = nc.sync if n == 0 else nc.gpsimd
-                    queue.dma_start(out=xa_n[g0:P:4, :], in_=xf[n, :, SIDE * i1 : SIDE * i1 + LEN])
                     queue.dma_start(out=xb_n[g0:P:4, :], in_=xf[n, :, SIDE * j1 : SIDE * j1 + LEN])
+            if n == 0:
+                for k, w in enumerate(PLAIN_WINDOWS):
+                    for i1 in range(2):
+                        for j1 in range(2):
+                            g0 = 2 * i1 + j1
+                            a0 = SIDE * (WROWS * w + i1)
+                            nc.sync.dma_start(
+                                out=xa_part[g0:P:4, :, k, 0:458],
+                                in_=xf[:, :, a0 : a0 + 458].rearrange("n c q -> c n q"),
+                            )
 
         gs = []
         for k in range(NG + NGP):
@@ -130,7 +143,7 @@ def tile_fast2order_de_conv_t_kernel(tc, x, W, out):
                     "n": n,
                     "y0": y0,
                     "kind": "small",
-                    "pe": False,
+                    "pe": True,
                     "slot": n % 2,
                     "first": k == 0,
                     "last": k == len(wins) - 1,
@@ -146,7 +159,7 @@ def tile_fast2order_de_conv_t_kernel(tc, x, W, out):
                     else:
                         win["kind"] = "dve"
                         win["slot"] = ndve % NG
-                        win["pe"] = (ndve * PE_WINDOWS) % (36 - len(GP_WINDOWS)) < PE_WINDOWS
+                        win["pe"] = y0 // WROWS not in PLAIN_WINDOWS
                         ndve += 1
                     nfull += 1
                 plan.append(win)
@@ -163,11 +176,11 @@ def tile_fast2order_de_conv_t_kernel(tc, x, W, out):
             xad_flat = None
             if win["pe"]:
                 xad = psum_x.tile([P, 2 * SLOT, 2], BF16, name="xad")
-                for r0, r1 in ((0, SLOT), (SLOT, 2 * m + 1)):
+                for r0, r1 in ((0, 2 * m + 1),) if small else ((0, SLOT), (SLOT, 2 * m + 1)):
                     nc.tensor.matmul(
                         out=xad[:, r0:r1, :],
-                        lhsT=ident[:],
-                        rhs=xas[n][:, q0 + r0 : q0 + r1].unsqueeze(2).to_broadcast([P, r1 - r0, 2]),
+                        lhsT=swap[:],
+                        rhs=xbs[n][:, q0 + r0 : q0 + r1].unsqueeze(2).to_broadcast([P, r1 - r0, 2]),
                         start=True,
                         stop=True,
                     )
@@ -179,7 +192,7 @@ def tile_fast2order_de_conv_t_kernel(tc, x, W, out):
                     )
                 else:
                     in0 = (
-                        xas[n][:, q0 + s : q0 + s + 2 * m]
+                        xa_part[:, n, PLAIN_WINDOWS.index(win["y0"] // WROWS), s : s + 2 * m]
                         .rearrange("p (m i) -> p m i", i=2)
                         .unsqueeze(3)
                         .to_broadcast([P, m, 2, 2])

@@ -243,12 +243,13 @@ def tile_fast2order_de_conv_t_kernel(tc, x, W, out):
                     )
                 else:
                     nc.scalar.copy(
-                        out=st[:, mt, b0 + 63 : b0 + 63 + 384]
-                        .rearrange("p (rho e) -> p rho e", e=128)[:, :, 0:66]
+                        out=st[:, mt, b0 + 64 : b0 + 64 + 384]
+                        .rearrange("p (rho e) -> p rho e", e=128)[:, :, 0:64]
                         .rearrange("p rho (k s) -> p rho k s", s=2),
-                        in_=ps[:, :, 32:227].rearrange("p s (rho k) -> p rho k s", k=65)[
-                            :, :, 0:33, :
-                        ],
+                        in_=ps[:]
+                        .rearrange("p s k -> p (s k)")[:, 0:510]
+                        .rearrange("p (e x) -> p e x", x=255)[:, ::-1, 33:228]
+                        .rearrange("p e (rho k) -> p rho k e", k=65)[:, :, 0:32, :],
                     )
                     nc.scalar.copy(
                         out=st[:, mt, b0 : b0 + 384]

@@ -52,15 +52,24 @@ def tile_fast2order_de_conv_t_kernel(tc, x, W, out):
         nc.sync.dma_start(out=w_sb[:], in_=W.rearrange("(ob o) f -> o ob f", o=P))
         xf = x.rearrange("n c h w -> n c (h w)")
         xbs = []
+        xbos = []
         xa_part = const.tile([P, B, len(PLAIN_WINDOWS), XAW], BF16, name="xa_part")
         for n in range(B):
             xb_n = const.tile([P, LEN], BF16, name="xb%d" % n)
             xbs.append(xb_n)
+            xbo_n = const.tile([P, LEN], BF16, name="xbo%d" % n)
+            xbos.append(xbo_n)
+            queue = nc.sync if n == 0 else nc.gpsimd
             for i1 in range(2):
                 for j1 in range(2):
                     g0 = 2 * i1 + j1
-                    queue = nc.sync if n == 0 else nc.gpsimd
                     queue.dma_start(out=xb_n[g0:P:4, :], in_=xf[n, :, SIDE * j1 : SIDE * j1 + LEN])
+            for i1 in range(2):
+                for j1 in range(2):
+                    g0 = 2 * i1 + j1
+                    queue.dma_start(
+                        out=xbo_n[g0:P:4, 0 : LEN - 1], in_=xf[n, :, SIDE * j1 + 1 : SIDE * j1 + LEN]
+                    )
             if n == 0:
                 for k, w in enumerate(PLAIN_WINDOWS):
                     for i1 in range(2):
@@ -197,8 +206,9 @@ def tile_fast2order_de_conv_t_kernel(tc, x, W, out):
                         .unsqueeze(3)
                         .to_broadcast([P, m, 2, 2])
                     )
+                start = q0 + s
                 in1 = (
-                    xbs[n][:, q0 + s : q0 + s + 2 * m]
+                    (xbs[n][:, start : start + 2 * m] if start % 2 == 0 else xbos[n][:, start - 1 : start - 1 + 2 * m])
                     .rearrange("p (m j) -> p m j", j=2)
                     .unsqueeze(2)
                     .to_broadcast([P, m, 2, 2])

@@ -26,6 +26,7 @@ NG = 4
 NGP = 0
 GP_WINDOWS = ()
 PLAIN_WINDOWS = (3, 7)
+XBO_PIECES = {0: (0, 1366), 4: (1820, 3186), 8: (3640, 4158)}
 XAW = 464
 STAGE = 22 * GRID
 FLOPS = 2 * O * F * B * L
@@ -64,12 +65,6 @@ def tile_fast2order_de_conv_t_kernel(tc, x, W, out):
                 for j1 in range(2):
                     g0 = 2 * i1 + j1
                     queue.dma_start(out=xb_n[g0:P:4, :], in_=xf[n, :, SIDE * j1 : SIDE * j1 + LEN])
-            for i1 in range(2):
-                for j1 in range(2):
-                    g0 = 2 * i1 + j1
-                    queue.dma_start(
-                        out=xbo_n[g0:P:4, 0 : LEN - 1], in_=xf[n, :, SIDE * j1 + 1 : SIDE * j1 + LEN]
-                    )
             if n == 0:
                 for k, w in enumerate(PLAIN_WINDOWS):
                     for i1 in range(2):
@@ -208,7 +203,7 @@ def tile_fast2order_de_conv_t_kernel(tc, x, W, out):
                     )
                 start = q0 + s
                 in1 = (
-                    (xbs[n][:, start : start + 2 * m] if start % 2 == 0 else xbos[n][:, start - 1 : start - 1 + 2 * m])
+                    (xbs[n][:, start : start + 2 * m] if start % 2 == 0 or not win["pe"] else xbos[n][:, start - 1 : start - 1 + 2 * m])
                     .rearrange("p (m j) -> p m j", j=2)
                     .unsqueeze(2)
                     .to_broadcast([P, m, 2, 2])
@@ -285,8 +280,19 @@ def tile_fast2order_de_conv_t_kernel(tc, x, W, out):
 
         for win in gp_wins[0:NGP]:
             emit_products(win)
+        def emit_shifted(win):
+            piece = XBO_PIECES.get(win["y0"] // WROWS) if win["kind"] == "dve" else None
+            if piece is not None:
+                nc.vector.tensor_copy(
+                    out=xbos[win["n"]][:, piece[0] : piece[1]], in_=xbs[win["n"]][:, piece[0] + 1 : piece[1] + 1]
+                )
+
         prev = None
-        for win in plan:
+        emit_shifted(plan[0])
+        emit_shifted(plan[1])
+        for k, win in enumerate(plan):
+            if k + 2 < len(plan):
+                emit_shifted(plan[k + 2])
             if win["kind"] != "gp":
                 emit_products(win)
             if prev is not None:

@@ -14,22 +14,20 @@ P = 128
 B = 4
 C = 32
 SIDE = 65
-IMG = SIDE * SIDE
 GRID = 64
-L = GRID * GRID
 O = 512
 F = 512
 LEN = GRID * SIDE
 SLOT = 256
 WROWS = 7
+HALF = 228
 NG = 4
-NGP = 0
-GP_WINDOWS = ()
 PLAIN_WINDOWS = (3, 7)
 XBO_PIECES = {0: (0, 1366), 4: (1820, 3186), 8: (3640, 4158)}
 XAW = 464
 STAGE = 22 * GRID
-FLOPS = 2 * O * F * B * L
+HELP = 4
+FLOPS = 2 * O * F * B * GRID * GRID
 
 
 def tile_fast2order_de_conv_t_kernel(tc, x, W, out):
@@ -50,7 +48,8 @@ def tile_fast2order_de_conv_t_kernel(tc, x, W, out):
         )
 
         w_sb = const.tile([P, 4, F], BF16, name="w_sb")
-        nc.sync.dma_start(out=w_sb[:], in_=W.rearrange("(ob o) f -> o ob f", o=P))
+        for ob in range(4):
+            nc.sync.dma_start(out=w_sb[:, ob, :], in_=W[ob * P : (ob + 1) * P, :])
         xf = x.rearrange("n c h w -> n c (h w)")
         xbs = []
         xbos = []
@@ -61,25 +60,22 @@ def tile_fast2order_de_conv_t_kernel(tc, x, W, out):
             xbo_n = const.tile([P, LEN], BF16, name="xbo%d" % n)
             xbos.append(xbo_n)
             queue = nc.sync if n == 0 else nc.gpsimd
-            for i1 in range(2):
-                for j1 in range(2):
-                    g0 = 2 * i1 + j1
-                    queue.dma_start(out=xb_n[g0:P:4, :], in_=xf[n, :, SIDE * j1 : SIDE * j1 + LEN])
+            for g0 in range(4):
+                j1 = g0 % 2
+                queue.dma_start(out=xb_n[g0:P:4, :], in_=xf[n, :, SIDE * j1 : SIDE * j1 + LEN])
             if n == 0:
                 for k, w in enumerate(PLAIN_WINDOWS):
-                    for i1 in range(2):
-                        for j1 in range(2):
-                            g0 = 2 * i1 + j1
-                            a0 = SIDE * (WROWS * w + i1)
-                            nc.sync.dma_start(
-                                out=xa_part[g0:P:4, :, k, 0:458],
-                                in_=xf[:, :, a0 : a0 + 458].rearrange("n c q -> c n q"),
-                            )
+                    for g0 in range(4):
+                        a0 = SIDE * (WROWS * w + g0 // 2)
+                        nc.sync.dma_start(
+                            out=xa_part[g0:P:4, :, k, 0:458],
+                            in_=xf[:, :, a0 : a0 + 458].rearrange("n c q -> c n q"),
+                        )
 
         gs = []
-        for k in range(NG + NGP):
+        for k in range(NG):
             gt = const.tile([P, 2, SLOT, 4], BF16, name="g%d" % k, align_bytes=64)
-            nc.vector.memset(gt[:, :, 228:SLOT, :], 0.0)
+            nc.vector.memset(gt[:, :, HALF:SLOT, :], 0.0)
             gs.append(gt)
         gsmall = []
         for k in range(2):
@@ -87,37 +83,32 @@ def tile_fast2order_de_conv_t_kernel(tc, x, W, out):
             gsmall.append(gt)
 
         w_perm = const.tile([P, 4, 4, P], BF16, name="w_perm")
-        wv = w_sb[:].rearrange(
-            "o ob (c i1 i0 j1 j0) -> o i0 j0 ob c i1 j1", c=C, i1=2, i0=2, j1=2, j0=2
-        )
-        for i0 in range(2):
-            for j0 in range(2):
-                nc.vector.tensor_copy(
-                    out=w_perm[:, :, 2 * i0 + j0, :].rearrange(
-                        "o ob (c i1 j1) -> o ob c i1 j1", c=C, i1=2, j1=2
-                    ),
-                    in_=wv[:, i0, j0],
-                )
         wg = const.tile([P, O, 4], BF16, name="wg", align_bytes=64)
+        w_codes = const.tile([P, O], U32, name="w_codes", align_bytes=64)
+        w_scales = const.tile([P, O], U8, name="w_scales", align_bytes=64)
         for ob in range(4):
+            wv = w_sb[:, ob, :].rearrange(
+                "o (ci i0 j1 j0) -> o i0 j0 ci j1", i0=2, j1=2, j0=2
+            )
+            for i0 in range(2):
+                copy = nc.vector.tensor_copy if i0 == 0 else nc.scalar.copy
+                copy(
+                    out=w_perm[:, ob, 2 * i0 : 2 * i0 + 2, :].rearrange(
+                        "o j0 (ci j1) -> o j0 ci j1", j1=2
+                    ),
+                    in_=wv[:, i0],
+                )
             xt = psum.tile([P, 4, P], BF16, name="xt", tag="bank")
             for t in range(4):
                 nc.tensor.transpose(xt[:, t, :], w_perm[:, ob, t, :], ident[:])
-            if ob % 2 == 0:
-                nc.vector.tensor_copy(
-                    out=wg[:, ob * P : (ob + 1) * P, :], in_=xt[:].rearrange("p t o -> p o t")
-                )
-            else:
-                nc.scalar.copy(
-                    out=wg[:, ob * P : (ob + 1) * P, :], in_=xt[:].rearrange("p t o -> p o t")
-                )
-        w_codes = const.tile([P, O], U32, name="w_codes", align_bytes=64)
-        w_scales = const.tile([P, O], U8, name="w_scales", align_bytes=64)
-        nc.vector.quantize_mx(
-            out=w_codes[:].bitcast(FP8X4),
-            scales=w_scales[:],
-            in_=wg[:].rearrange("p o t -> p (o t)"),
-        )
+            cols = slice(ob * P, (ob + 1) * P)
+            copy = nc.vector.tensor_copy if ob % 2 == 0 else nc.scalar.copy
+            copy(out=wg[:, cols, :], in_=xt[:].rearrange("p t o -> p o t"))
+            nc.vector.quantize_mx(
+                out=w_codes[:, cols].bitcast(FP8X4),
+                scales=w_scales[:, cols],
+                in_=wg[:, cols, :].rearrange("p o t -> p (o t)"),
+            )
 
         out_v = out.rearrange("n (mt o) y z -> n mt o (y z)", o=P)
 
@@ -134,49 +125,52 @@ def tile_fast2order_de_conv_t_kernel(tc, x, W, out):
             if n < B - 1:
                 chunks.append((n, full[6:9] + [last]))
             else:
-                chunks.append((n, full[6:8]))
-                chunks.append((n, full[8:9] + [last]))
+                chunks.append((n, full[6:7]))
+                chunks.append((n, full[7:8]))
+                chunks.append((n, full[8:9]))
+                chunks.append((n, [last]))
 
         plan = []
-        gp_wins = []
         nfull = 0
-        ndve = 0
         for n, wins in chunks:
             for k, (y0, nrows) in enumerate(wins):
-                win = {
-                    "n": n,
-                    "y0": y0,
-                    "kind": "small",
-                    "pe": True,
-                    "slot": n % 2,
-                    "first": k == 0,
-                    "last": k == len(wins) - 1,
-                    "row_first": wins[0][0],
-                    "rows": sum(w[1] for w in wins),
-                }
-                if nrows == WROWS:
-                    if nfull in GP_WINDOWS:
-                        win["kind"] = "gp"
-                        win["slot"] = NG + len(gp_wins) % NGP
-                        win["order"] = len(gp_wins)
-                        gp_wins.append(win)
-                    else:
-                        win["kind"] = "dve"
-                        win["slot"] = ndve % NG
-                        win["pe"] = y0 // WROWS not in PLAIN_WINDOWS
-                        ndve += 1
+                small = nrows != WROWS
+                plan.append(
+                    {
+                        "n": n,
+                        "y0": y0,
+                        "small": small,
+                        "pe": small or y0 // WROWS not in PLAIN_WINDOWS,
+                        "slot": n % 2 if small else nfull % NG,
+                        "first": k == 0,
+                        "last": k == len(wins) - 1,
+                        "row_first": wins[0][0],
+                        "rows": sum(w[1] for w in wins),
+                        "help": False,
+                    }
+                )
+                if not small:
                     nfull += 1
-                plan.append(win)
+        for win in plan[len(plan) - HELP :]:
+            win["help"] = True
 
         state = {}
+        deferred = []
+
+        def emit_shifted(win):
+            piece = None if win["small"] else XBO_PIECES.get(win["y0"] // WROWS)
+            if piece is not None:
+                nc.vector.tensor_copy(
+                    out=xbos[win["n"]][:, piece[0] : piece[1]],
+                    in_=xbs[win["n"]][:, piece[0] + 1 : piece[1] + 1],
+                )
 
         def emit_products(win):
             n = win["n"]
             q0 = SIDE * win["y0"]
-            small = win["kind"] == "small"
-            m = 32 if small else 228
+            small = win["small"]
+            m = 32 if small else HALF
             gt = gsmall[win["slot"]] if small else gs[win["slot"]]
-            eng = nc.gpsimd if win["kind"] == "gp" else nc.vector
             xad_flat = None
             if win["pe"]:
                 xad = psum_x.tile([P, 2 * SLOT, 2], BF16, name="xad")
@@ -202,20 +196,51 @@ def tile_fast2order_de_conv_t_kernel(tc, x, W, out):
                         .to_broadcast([P, m, 2, 2])
                     )
                 start = q0 + s
+                if start % 2 == 0 or not win["pe"]:
+                    pairs = xbs[n][:, start : start + 2 * m]
+                else:
+                    pairs = xbos[n][:, start - 1 : start - 1 + 2 * m]
                 in1 = (
-                    (xbs[n][:, start : start + 2 * m] if start % 2 == 0 or not win["pe"] else xbos[n][:, start - 1 : start - 1 + 2 * m])
-                    .rearrange("p (m j) -> p m j", j=2)
-                    .unsqueeze(2)
-                    .to_broadcast([P, m, 2, 2])
+                    pairs.rearrange("p (m j) -> p m j", j=2).unsqueeze(2).to_broadcast([P, m, 2, 2])
                 )
                 dst = gt[:, s * m : (s + 1) * m, :] if small else gt[:, s, 0:m, :]
-                eng.tensor_tensor(
+                nc.vector.tensor_tensor(
                     out=dst.rearrange("p m (i j) -> p m i j", i=2), in0=in0, in1=in1, op=MULT
                 )
 
+        def evacuate(copy, ps, st, mt, b0, small):
+            if small:
+                copy(
+                    out=st[:, mt, b0 : b0 + GRID].rearrange("p (a s) -> p a s", s=2),
+                    in_=ps[:].rearrange("p s a -> p a s"),
+                )
+                return
+            copy(
+                out=st[:, mt, b0 + 64 : b0 + 64 + 384]
+                .rearrange("p (rho e) -> p rho e", e=128)[:, :, 0:64]
+                .rearrange("p rho (k s) -> p rho k s", s=2),
+                in_=ps[:]
+                .rearrange("p s k -> p (s k)")[:, 0:510]
+                .rearrange("p (e x) -> p e x", x=255)[:, ::-1, 33:228]
+                .rearrange("p e (rho k) -> p rho k e", k=65)[:, :, 0:32, :],
+            )
+            copy(
+                out=st[:, mt, b0 : b0 + 384]
+                .rearrange("p (rho e) -> p rho e", e=128)[:, :, 0:64]
+                .rearrange("p rho (a s) -> p rho a s", s=2),
+                in_=ps[:, :, 0:195].rearrange("p s (rho k) -> p rho k s", k=65)[:, :, 0:32, :],
+            )
+            copy(
+                out=st[:, mt, b0 + 384 : b0 + 448].rearrange("p (a s) -> p a s", s=2),
+                in_=ps[:, :, 195:227].rearrange("p s a -> p a s"),
+            )
+
+        def store(n, st, pos0, size):
+            for mt in range(4):
+                nc.sync.dma_start(out=out_v[n, mt][:, pos0 : pos0 + size], in_=st[:, mt, 0:size])
+
         def emit_rest(win):
-            n = win["n"]
-            small = win["kind"] == "small"
+            small = win["small"]
             width = GRID if small else 2 * SLOT
             if small:
                 g_flat = gsmall[win["slot"]][:].rearrange("p m t -> p (m t)")
@@ -241,51 +266,15 @@ def tile_fast2order_de_conv_t_kernel(tc, x, W, out):
                     start=True,
                     stop=True,
                 )
-                if small:
-                    nc.scalar.copy(
-                        out=st[:, mt, b0 : b0 + GRID].rearrange("p (a s) -> p a s", s=2),
-                        in_=ps[:].rearrange("p s a -> p a s"),
-                    )
+                if win["help"] and mt % 2 == 1:
+                    deferred.append(("copy", ps, st, mt, b0, small))
                 else:
-                    nc.scalar.copy(
-                        out=st[:, mt, b0 + 64 : b0 + 64 + 384]
-                        .rearrange("p (rho e) -> p rho e", e=128)[:, :, 0:64]
-                        .rearrange("p rho (k s) -> p rho k s", s=2),
-                        in_=ps[:]
-                        .rearrange("p s k -> p (s k)")[:, 0:510]
-                        .rearrange("p (e x) -> p e x", x=255)[:, ::-1, 33:228]
-                        .rearrange("p e (rho k) -> p rho k e", k=65)[:, :, 0:32, :],
-                    )
-                    nc.scalar.copy(
-                        out=st[:, mt, b0 : b0 + 384]
-                        .rearrange("p (rho e) -> p rho e", e=128)[:, :, 0:64]
-                        .rearrange("p rho (a s) -> p rho a s", s=2),
-                        in_=ps[:, :, 0:195].rearrange("p s (rho k) -> p rho k s", k=65)[
-                            :, :, 0:32, :
-                        ],
-                    )
-                    nc.scalar.copy(
-                        out=st[:, mt, b0 + 384 : b0 + 448].rearrange("p (a s) -> p a s", s=2),
-                        in_=ps[:, :, 195:227].rearrange("p s a -> p a s"),
-                    )
+                    evacuate(nc.scalar.copy, ps, st, mt, b0, small)
             if win["last"]:
-                size = GRID * win["rows"]
-                pos0 = GRID * win["row_first"]
-                for mt in range(4):
-                    nc.sync.dma_start(
-                        out=out_v[n, mt][:, pos0 : pos0 + size], in_=st[:, mt, 0:size]
-                    )
-            if win["kind"] == "gp" and win["order"] + NGP < len(gp_wins):
-                emit_products(gp_wins[win["order"] + NGP])
-
-        for win in gp_wins[0:NGP]:
-            emit_products(win)
-        def emit_shifted(win):
-            piece = XBO_PIECES.get(win["y0"] // WROWS) if win["kind"] == "dve" else None
-            if piece is not None:
-                nc.vector.tensor_copy(
-                    out=xbos[win["n"]][:, piece[0] : piece[1]], in_=xbs[win["n"]][:, piece[0] + 1 : piece[1] + 1]
-                )
+                if win["help"]:
+                    deferred.append(("store", win["n"], st, GRID * win["row_first"], GRID * win["rows"]))
+                else:
+                    store(win["n"], st, GRID * win["row_first"], GRID * win["rows"])
 
         prev = None
         emit_shifted(plan[0])
@@ -293,9 +282,13 @@ def tile_fast2order_de_conv_t_kernel(tc, x, W, out):
         for k, win in enumerate(plan):
             if k + 2 < len(plan):
                 emit_shifted(plan[k + 2])
-            if win["kind"] != "gp":
-                emit_products(win)
+            emit_products(win)
             if prev is not None:
                 emit_rest(prev)
             prev = win
         emit_rest(prev)
+        for item in deferred:
+            if item[0] == "copy":
+                evacuate(nc.vector.tensor_copy, item[1], item[2], item[3], item[4], item[5])
+            else:
+                store(item[1], item[2], item[3], item[4])

@@ -22,9 +22,9 @@ SLOT = 256
 WROWS = 7
 HALF = 228
 NG = 4
-PLAIN_WINDOWS = (3, 7)
-XBO_PIECES = {0: (0, 1366), 4: (1820, 3186), 8: (3640, 4158)}
-XAW = 464
+PLAIN_WINDOWS = (4, 5)
+XBO_PIECES = {0: (0, 1820), 6: (2730, 4158)}
+XAW = 928
 STAGE = 22 * GRID
 HELP = 4
 FLOPS = 2 * O * F * B * GRID * GRID
@@ -53,7 +53,12 @@ def tile_fast2order_de_conv_t_kernel(tc, x, W, out):
         xf = x.rearrange("n c h w -> n c (h w)")
         xbs = []
         xbos = []
-        xa_part = const.tile([P, B, len(PLAIN_WINDOWS), XAW], BF16, name="xa_part")
+        xa_part = const.tile([P, B, XAW], BF16, name="xa_part")
+        for g0 in range(4):
+            a0 = SIDE * (WROWS * PLAIN_WINDOWS[0] + g0 // 2)
+            nc.gpsimd.dma_start(
+                out=xa_part[g0:P:4, :, 0:912], in_=xf[:, :, a0 : a0 + 912].rearrange("n c q -> c n q")
+            )
         for n in range(B):
             xb_n = const.tile([P, LEN], BF16, name="xb%d" % n)
             xbs.append(xb_n)
@@ -63,14 +68,6 @@ def tile_fast2order_de_conv_t_kernel(tc, x, W, out):
             for g0 in range(4):
                 j1 = g0 % 2
                 queue.dma_start(out=xb_n[g0:P:4, :], in_=xf[n, :, SIDE * j1 : SIDE * j1 + LEN])
-            if n == 0:
-                for k, w in enumerate(PLAIN_WINDOWS):
-                    for g0 in range(4):
-                        a0 = SIDE * (WROWS * w + g0 // 2)
-                        nc.sync.dma_start(
-                            out=xa_part[g0:P:4, :, k, 0:458],
-                            in_=xf[:, :, a0 : a0 + 458].rearrange("n c q -> c n q"),
-                        )
 
         gs = []
         for k in range(NG):
@@ -189,8 +186,9 @@ def tile_fast2order_de_conv_t_kernel(tc, x, W, out):
                         "p (m i j) -> p m i j", i=2, j=2
                     )
                 else:
+                    local = q0 - SIDE * WROWS * PLAIN_WINDOWS[0] + s
                     in0 = (
-                        xa_part[:, n, PLAIN_WINDOWS.index(win["y0"] // WROWS), s : s + 2 * m]
+                        xa_part[:, n, local : local + 2 * m]
                         .rearrange("p (m i) -> p m i", i=2)
                         .unsqueeze(3)
                         .to_broadcast([P, m, 2, 2])

@@ -23,10 +23,10 @@ WROWS = 7
 HALF = 228
 NG = 4
 PLAIN_WINDOWS = (4, 5)
-XBO_PIECES = {0: (0, 1820), 6: (2730, 4158)}
+XBO_PIECES = {0: (0, 1820), 4: (1820, 2730), 6: (2730, 4158)}
 XAW = 928
 STAGE = 22 * GRID
-HELP = 4
+HELP = 0
 FLOPS = 2 * O * F * B * GRID * GRID
 
 
@@ -57,7 +57,7 @@ def tile_fast2order_de_conv_t_kernel(tc, x, W, out):
         for g0 in range(4):
             a0 = SIDE * (WROWS * PLAIN_WINDOWS[0] + g0 // 2)
             nc.gpsimd.dma_start(
-                out=xa_part[g0:P:4, :, 0:912], in_=xf[:, :, a0 : a0 + 912].rearrange("n c q -> c n q")
+                out=xa_part[g0:P:4, :, 0:914], in_=xf[:, :, a0 : a0 + 914].rearrange("n c q -> c n q")
             )
         for n in range(B):
             xb_n = const.tile([P, LEN], BF16, name="xb%d" % n)
@@ -74,6 +74,10 @@ def tile_fast2order_de_conv_t_kernel(tc, x, W, out):
             gt = const.tile([P, 2, SLOT, 4], BF16, name="g%d" % k, align_bytes=64)
             nc.vector.memset(gt[:, :, HALF:SLOT, :], 0.0)
             gs.append(gt)
+        xa2s = []
+        for k in range(2):
+            xa2 = const.tile([P, 458, 2], BF16, name="xa2_%d" % k)
+            xa2s.append(xa2)
         gsmall = []
         for k in range(2):
             gt = const.tile([P, GRID, 4], BF16, name="gsmall%d" % k, align_bytes=64)
@@ -122,10 +126,8 @@ def tile_fast2order_de_conv_t_kernel(tc, x, W, out):
             if n < B - 1:
                 chunks.append((n, full[6:9] + [last]))
             else:
-                chunks.append((n, full[6:7]))
-                chunks.append((n, full[7:8]))
-                chunks.append((n, full[8:9]))
-                chunks.append((n, [last]))
+                chunks.append((n, full[6:8]))
+                chunks.append((n, full[8:9] + [last]))
 
         plan = []
         nfull = 0
@@ -161,6 +163,12 @@ def tile_fast2order_de_conv_t_kernel(tc, x, W, out):
                     out=xbos[win["n"]][:, piece[0] : piece[1]],
                     in_=xbs[win["n"]][:, piece[0] + 1 : piece[1] + 1],
                 )
+            if not win["pe"]:
+                local = SIDE * (win["y0"] - WROWS * PLAIN_WINDOWS[0])
+                nc.vector.tensor_copy(
+                    out=xa2s[(win["y0"] // WROWS) % 2][:],
+                    in_=xa_part[:, win["n"], local : local + 458].unsqueeze(2).to_broadcast([P, 458, 2]),
+                )
 
         def emit_products(win):
             n = win["n"]
@@ -180,21 +188,12 @@ def tile_fast2order_de_conv_t_kernel(tc, x, W, out):
                         stop=True,
                     )
                 xad_flat = xad[:].rearrange("p r e -> p (r e)")
+            else:
+                xad_flat = xa2s[(win["y0"] // WROWS) % 2][:].rearrange("p r e -> p (r e)")
             for s in range(2):
-                if win["pe"]:
-                    in0 = xad_flat[:, 2 * s : 2 * s + 4 * m].rearrange(
-                        "p (m i j) -> p m i j", i=2, j=2
-                    )
-                else:
-                    local = q0 - SIDE * WROWS * PLAIN_WINDOWS[0] + s
-                    in0 = (
-                        xa_part[:, n, local : local + 2 * m]
-                        .rearrange("p (m i) -> p m i", i=2)
-                        .unsqueeze(3)
-                        .to_broadcast([P, m, 2, 2])
-                    )
+                in0 = xad_flat[:, 2 * s : 2 * s + 4 * m].rearrange("p (m i j) -> p m i j", i=2, j=2)
                 start = q0 + s
-                if start % 2 == 0 or not win["pe"]:
+                if start % 2 == 0:
                     pairs = xbs[n][:, start : start + 2 * m]
                 else:
                     pairs = xbos[n][:, start - 1 : start - 1 + 2 * m]

@@ -24,9 +24,11 @@ HALF = 228
 NG = 4
 PLAIN_WINDOWS = (4, 5)
 XBO_PIECES = {0: (0, 1820), 4: (1820, 2730), 6: (2730, 4158)}
+SYNC_IMAGES = 2
 XAW = 928
 STAGE = 22 * GRID
 HELP = 0
+LEND = ((0, 6), (1, 6), (2, 6), (3, 3))
 FLOPS = 2 * O * F * B * GRID * GRID
 
 
@@ -64,7 +66,7 @@ def tile_fast2order_de_conv_t_kernel(tc, x, W, out):
             xbs.append(xb_n)
             xbo_n = const.tile([P, LEN], BF16, name="xbo%d" % n)
             xbos.append(xbo_n)
-            queue = nc.sync if n == 0 else nc.gpsimd
+            queue = nc.sync if n <= SYNC_IMAGES else nc.gpsimd
             for g0 in range(4):
                 j1 = g0 % 2
                 queue.dma_start(out=xb_n[g0:P:4, :], in_=xf[n, :, SIDE * j1 : SIDE * j1 + LEN])
@@ -154,6 +156,7 @@ def tile_fast2order_de_conv_t_kernel(tc, x, W, out):
             win["help"] = True
 
         state = {}
+        late = []
         deferred = []
 
         def emit_shifted(win):
@@ -263,7 +266,9 @@ def tile_fast2order_de_conv_t_kernel(tc, x, W, out):
                     start=True,
                     stop=True,
                 )
-                if win["help"] and mt % 2 == 1:
+                if mt == 3 and (win["n"], win["y0"] // WROWS) in LEND:
+                    late.append([2, ps, st, mt, b0])
+                elif win["help"] and mt % 2 == 1:
                     deferred.append(("copy", ps, st, mt, b0, small))
                 else:
                     evacuate(nc.scalar.copy, ps, st, mt, b0, small)
@@ -283,6 +288,10 @@ def tile_fast2order_de_conv_t_kernel(tc, x, W, out):
             if prev is not None:
                 emit_rest(prev)
             prev = win
+            for item in late:
+                item[0] -= 1
+                if item[0] == 0:
+                    evacuate(nc.vector.tensor_copy, item[1], item[2], item[3], item[4], False)
         emit_rest(prev)
         for item in deferred:
             if item[0] == "copy":

@@ -21,7 +21,7 @@ LEN = GRID * SIDE
 SLOT = 256
 WROWS = 7
 HALF = 228
-NG = 4
+NG = 5
 PLAIN_WINDOWS = (4, 5)
 XBO_PIECES = {0: (0, 1820), 4: (1820, 2730), 6: (2730, 4158)}
 SYNC_IMAGES = 2
@@ -36,7 +36,7 @@ def tile_fast2order_de_conv_t_kernel(tc, x, W, out):
     nc = tc.nc
     with ExitStack() as ctx:
         const = ctx.enter_context(tc.tile_pool(name="const", bufs=1))
-        cpool = ctx.enter_context(tc.tile_pool(name="cpool", bufs=3))
+        cpool = ctx.enter_context(tc.tile_pool(name="cpool", bufs=4))
         stage = ctx.enter_context(tc.tile_pool(name="stage", bufs=5))
         psum = ctx.enter_context(tc.psum_pool(name="psum", bufs=6))
         psum_x = ctx.enter_context(tc.psum_pool(name="psum_x", bufs=2))

@@ -26,9 +26,9 @@ PLAIN_WINDOWS = (4, 5)
 XBO_PIECES = {0: (0, 1820), 4: (1820, 2730), 6: (2730, 4158)}
 SYNC_IMAGES = 2
 XAW = 928
-STAGE = 22 * GRID
-HELP = 0
-LEND = ((0, 6), (1, 6), (2, 6), (3, 3))
+PERIOD = 4
+STAGE = (PERIOD * WROWS + 1) * GRID
+LEND = (3,)
 FLOPS = 2 * O * F * B * GRID * GRID
 
 
@@ -37,7 +37,7 @@ def tile_fast2order_de_conv_t_kernel(tc, x, W, out):
     with ExitStack() as ctx:
         const = ctx.enter_context(tc.tile_pool(name="const", bufs=1))
         cpool = ctx.enter_context(tc.tile_pool(name="cpool", bufs=4))
-        stage = ctx.enter_context(tc.tile_pool(name="stage", bufs=5))
+        stage = ctx.enter_context(tc.tile_pool(name="stage", bufs=14))
         psum = ctx.enter_context(tc.psum_pool(name="psum", bufs=6))
         psum_x = ctx.enter_context(tc.psum_pool(name="psum_x", bufs=2))
 
@@ -115,49 +115,32 @@ def tile_fast2order_de_conv_t_kernel(tc, x, W, out):
 
         out_v = out.rearrange("n (mt o) y z -> n mt o (y z)", o=P)
 
-        full = [(WROWS * w, WROWS) for w in range(9)]
-        last = (63, 1)
-        chunks = []
-        for n in range(B):
-            if n == 0:
-                chunks.append((n, full[0:1]))
-                chunks.append((n, full[1:3]))
-            else:
-                chunks.append((n, full[0:3]))
-            chunks.append((n, full[3:6]))
-            if n < B - 1:
-                chunks.append((n, full[6:9] + [last]))
-            else:
-                chunks.append((n, full[6:8]))
-                chunks.append((n, full[8:9] + [last]))
-
         plan = []
         nfull = 0
-        for n, wins in chunks:
-            for k, (y0, nrows) in enumerate(wins):
-                small = nrows != WROWS
+        for n in range(B):
+            for w in range(10):
+                small = w == 9
                 plan.append(
                     {
                         "n": n,
-                        "y0": y0,
+                        "w": w,
+                        "y0": WROWS * w,
                         "small": small,
-                        "pe": small or y0 // WROWS not in PLAIN_WINDOWS,
+                        "pe": small or w not in PLAIN_WINDOWS,
                         "slot": n % 2 if small else nfull % NG,
-                        "first": k == 0,
-                        "last": k == len(wins) - 1,
-                        "row_first": wins[0][0],
-                        "rows": sum(w[1] for w in wins),
-                        "help": False,
                     }
                 )
                 if not small:
                     nfull += 1
-        for win in plan[len(plan) - HELP :]:
-            win["help"] = True
+
+        def piece_starts(w, mt):
+            return w == 0 or (w < 9 and (w - mt) % PERIOD == 0)
+
+        def piece_ends(w, mt):
+            return w == 9 or (w < 8 and (w - mt) % PERIOD == PERIOD - 1)
 
         state = {}
         late = []
-        deferred = []
 
         def emit_shifted(win):
             piece = None if win["small"] else XBO_PIECES.get(win["y0"] // WROWS)
@@ -208,15 +191,15 @@ def tile_fast2order_de_conv_t_kernel(tc, x, W, out):
                     out=dst.rearrange("p m (i j) -> p m i j", i=2), in0=in0, in1=in1, op=MULT
                 )
 
-        def evacuate(copy, ps, st, mt, b0, small):
+        def evacuate(copy, ps, st, b0, small):
             if small:
                 copy(
-                    out=st[:, mt, b0 : b0 + GRID].rearrange("p (a s) -> p a s", s=2),
+                    out=st[:, b0 : b0 + GRID].rearrange("p (a s) -> p a s", s=2),
                     in_=ps[:].rearrange("p s a -> p a s"),
                 )
                 return
             copy(
-                out=st[:, mt, b0 + 64 : b0 + 64 + 384]
+                out=st[:, b0 + 64 : b0 + 64 + 384]
                 .rearrange("p (rho e) -> p rho e", e=128)[:, :, 0:64]
                 .rearrange("p rho (k s) -> p rho k s", s=2),
                 in_=ps[:]
@@ -225,19 +208,15 @@ def tile_fast2order_de_conv_t_kernel(tc, x, W, out):
                 .rearrange("p e (rho k) -> p rho k e", k=65)[:, :, 0:32, :],
             )
             copy(
-                out=st[:, mt, b0 : b0 + 384]
+                out=st[:, b0 : b0 + 384]
                 .rearrange("p (rho e) -> p rho e", e=128)[:, :, 0:64]
                 .rearrange("p rho (a s) -> p rho a s", s=2),
                 in_=ps[:, :, 0:195].rearrange("p s (rho k) -> p rho k s", k=65)[:, :, 0:32, :],
             )
             copy(
-                out=st[:, mt, b0 + 384 : b0 + 448].rearrange("p (a s) -> p a s", s=2),
+                out=st[:, b0 + 384 : b0 + 448].rearrange("p (a s) -> p a s", s=2),
                 in_=ps[:, :, 195:227].rearrange("p s a -> p a s"),
             )
-
-        def store(n, st, pos0, size):
-            for mt in range(4):
-                nc.sync.dma_start(out=out_v[n, mt][:, pos0 : pos0 + size], in_=st[:, mt, 0:size])
 
         def emit_rest(win):
             small = win["small"]
@@ -251,11 +230,13 @@ def tile_fast2order_de_conv_t_kernel(tc, x, W, out):
                 codes = cpool.tile([P, 2 * SLOT], U32, name="codes", align_bytes=64)
                 scales = cpool.tile([P, 2 * SLOT], U8, name="scales", align_bytes=64)
             nc.vector.quantize_mx(out=codes[:].bitcast(FP8X4), scales=scales[:], in_=g_flat)
-            if win["first"]:
-                state["st"] = stage.tile([P, 4, STAGE], F32, name="st")
-            st = state["st"]
-            b0 = (win["y0"] - win["row_first"]) * GRID
+            w = win["w"]
             for mt in range(4):
+                if piece_starts(w, mt):
+                    st = stage.tile([P, STAGE], F32, name="st")
+                    state[mt] = (st, win["y0"])
+                st, row_first = state[mt]
+                b0 = (win["y0"] - row_first) * GRID
                 ps = psum.tile([P, 2, width // 2], F32, name="ps", tag="bank")
                 nc.tensor.matmul_mx(
                     out=ps[:].rearrange("p s k -> p (s k)"),
@@ -266,17 +247,14 @@ def tile_fast2order_de_conv_t_kernel(tc, x, W, out):
                     start=True,
                     stop=True,
                 )
-                if mt == 3 and (win["n"], win["y0"] // WROWS) in LEND:
-                    late.append([2, ps, st, mt, b0])
-                elif win["help"] and mt % 2 == 1:
-                    deferred.append(("copy", ps, st, mt, b0, small))
+                if mt == 3 and w in LEND:
+                    late.append([2, ps, st, b0])
                 else:
-                    evacuate(nc.scalar.copy, ps, st, mt, b0, small)
-            if win["last"]:
-                if win["help"]:
-                    deferred.append(("store", win["n"], st, GRID * win["row_first"], GRID * win["rows"]))
-                else:
-                    store(win["n"], st, GRID * win["row_first"], GRID * win["rows"])
+                    evacuate(nc.scalar.copy, ps, st, b0, small)
+                if piece_ends(w, mt):
+                    size = b0 + (GRID if small else WROWS * GRID)
+                    pos0 = row_first * GRID
+                    nc.sync.dma_start(out=out_v[win["n"], mt][:, pos0 : pos0 + size], in_=st[:, 0:size])
 
         prev = None
         emit_shifted(plan[0])
@@ -291,10 +269,5 @@ def tile_fast2order_de_conv_t_kernel(tc, x, W, out):
             for item in late:
                 item[0] -= 1
                 if item[0] == 0:
-                    evacuate(nc.vector.tensor_copy, item[1], item[2], item[3], item[4], False)
+                    evacuate(nc.vector.tensor_copy, item[1], item[2], item[3], False)
         emit_rest(prev)
-        for item in deferred:
-            if item[0] == "copy":
-                evacuate(nc.vector.tensor_copy, item[1], item[2], item[3], item[4], item[5])
-            else:
-                store(item[1], item[2], item[3], item[4])

@@ -21,14 +21,14 @@ LEN = GRID * SIDE
 SLOT = 256
 WROWS = 7
 HALF = 228
-NG = 5
+NG = 4
 PLAIN_WINDOWS = (4, 5)
 XBO_PIECES = {0: (0, 1820), 4: (1820, 2730), 6: (2730, 4158)}
 SYNC_IMAGES = 2
 XAW = 928
 PERIOD = 4
 STAGE = (PERIOD * WROWS + 1) * GRID
-LEND = (3,)
+LEND = ((6, 2),)
 FLOPS = 2 * O * F * B * GRID * GRID
 
 
@@ -36,8 +36,10 @@ def tile_fast2order_de_conv_t_kernel(tc, x, W, out):
     nc = tc.nc
     with ExitStack() as ctx:
         const = ctx.enter_context(tc.tile_pool(name="const", bufs=1))
+        xpool = ctx.enter_context(tc.tile_pool(name="xpool", bufs=B))
+        opool = ctx.enter_context(tc.tile_pool(name="opool", bufs=2))
         cpool = ctx.enter_context(tc.tile_pool(name="cpool", bufs=4))
-        stage = ctx.enter_context(tc.tile_pool(name="stage", bufs=14))
+        stage = ctx.enter_context(tc.tile_pool(name="stage", bufs=18))
         psum = ctx.enter_context(tc.psum_pool(name="psum", bufs=6))
         psum_x = ctx.enter_context(tc.psum_pool(name="psum_x", bufs=2))
 
@@ -61,15 +63,16 @@ def tile_fast2order_de_conv_t_kernel(tc, x, W, out):
             nc.gpsimd.dma_start(
                 out=xa_part[g0:P:4, :, 0:914], in_=xf[:, :, a0 : a0 + 914].rearrange("n c q -> c n q")
             )
-        for n in range(B):
-            xb_n = const.tile([P, LEN], BF16, name="xb%d" % n)
-            xbs.append(xb_n)
-            xbo_n = const.tile([P, LEN], BF16, name="xbo%d" % n)
-            xbos.append(xbo_n)
-            queue = nc.sync if n <= SYNC_IMAGES else nc.gpsimd
+
+        def load_image(queue, n):
+            xb = xpool.tile([P, LEN], BF16, name="xb")
+            xbs.append(xb)
             for g0 in range(4):
                 j1 = g0 % 2
-                queue.dma_start(out=xb_n[g0:P:4, :], in_=xf[n, :, SIDE * j1 : SIDE * j1 + LEN])
+                queue.dma_start(out=xb[g0:P:4, :], in_=xf[n, :, SIDE * j1 : SIDE * j1 + LEN])
+
+        for n in range(B):
+            load_image(nc.sync if n <= SYNC_IMAGES else nc.gpsimd, n)
 
         gs = []
         for k in range(NG):
@@ -133,11 +136,13 @@ def tile_fast2order_de_conv_t_kernel(tc, x, W, out):
                 if not small:
                     nfull += 1
 
-        def piece_starts(w, mt):
-            return w == 0 or (w < 9 and (w - mt) % PERIOD == 0)
-
-        def piece_ends(w, mt):
+        def piece_ends(n, w, mt):
+            if w == 7 and n == B - 1:
+                return True
             return w == 9 or (w < 8 and (w - mt) % PERIOD == PERIOD - 1)
+
+        def piece_starts(n, w, mt):
+            return w == 0 or piece_ends(n, w - 1, mt)
 
         state = {}
         late = []
@@ -145,6 +150,9 @@ def tile_fast2order_de_conv_t_kernel(tc, x, W, out):
         def emit_shifted(win):
             piece = None if win["small"] else XBO_PIECES.get(win["y0"] // WROWS)
             if piece is not None:
+                if piece[0] == 0:
+                    xbo = opool.tile([P, LEN], BF16, name="xbo")
+                    xbos.append(xbo)
                 nc.vector.tensor_copy(
                     out=xbos[win["n"]][:, piece[0] : piece[1]],
                     in_=xbs[win["n"]][:, piece[0] + 1 : piece[1] + 1],
@@ -232,7 +240,7 @@ def tile_fast2order_de_conv_t_kernel(tc, x, W, out):
             nc.vector.quantize_mx(out=codes[:].bitcast(FP8X4), scales=scales[:], in_=g_flat)
             w = win["w"]
             for mt in range(4):
-                if piece_starts(w, mt):
+                if piece_starts(win["n"], w, mt):
                     st = stage.tile([P, STAGE], F32, name="st")
                     state[mt] = (st, win["y0"])
                 st, row_first = state[mt]
@@ -247,11 +255,11 @@ def tile_fast2order_de_conv_t_kernel(tc, x, W, out):
                     start=True,
                     stop=True,
                 )
-                if mt == 3 and w in LEND:
+                if (w, mt) in LEND and win["n"] < B - 1:
                     late.append([2, ps, st, b0])
                 else:
                     evacuate(nc.scalar.copy, ps, st, b0, small)
-                if piece_ends(w, mt):
+                if piece_ends(win["n"], w, mt):
                     size = b0 + (GRID if small else WROWS * GRID)
                     pos0 = row_first * GRID
                     nc.sync.dma_start(out=out_v[win["n"], mt][:, pos0 : pos0 + size], in_=st[:, 0:size])

@@ -24,9 +24,13 @@ HALF = 228
 NG = 4
 PLAIN_WINDOWS = (4, 5)
 XBO_PIECES = {0: (0, 1820), 4: (1820, 2730), 6: (2730, 4158)}
+XBO_PIECES_0 = {0: (0, 456), 1: (456, 1366), 3: (1366, 1820), 4: (1820, 2730), 6: (2730, 4158)}
+FIRST = 1376
+REST = 1364
 SYNC_IMAGES = 2
 XAW = 928
 PERIOD = 4
+HELP_FROM = 6
 STAGE = (PERIOD * WROWS + 1) * GRID
 LEND = ((6, 2),)
 FLOPS = 2 * O * F * B * GRID * GRID
@@ -35,8 +39,8 @@ FLOPS = 2 * O * F * B * GRID * GRID
 def tile_fast2order_de_conv_t_kernel(tc, x, W, out):
     nc = tc.nc
     with ExitStack() as ctx:
+        ctx.enter_context(tc.manual_schedule())
         const = ctx.enter_context(tc.tile_pool(name="const", bufs=1))
-        xpool = ctx.enter_context(tc.tile_pool(name="xpool", bufs=B))
         opool = ctx.enter_context(tc.tile_pool(name="opool", bufs=2))
         cpool = ctx.enter_context(tc.tile_pool(name="cpool", bufs=4))
         stage = ctx.enter_context(tc.tile_pool(name="stage", bufs=18))
@@ -46,14 +50,12 @@ def tile_fast2order_de_conv_t_kernel(tc, x, W, out):
         ident = const.tile([P, P], BF16, name="ident")
         make_identity(nc, ident[:])
         swap = const.tile([P, P], BF16, name="swap")
-        nc.vector.tensor_copy(
+        nc.gpsimd.tensor_copy(
             out=swap[:].rearrange("p (c a b) -> p c a b", c=C, a=2, b=2),
             in_=ident[:].rearrange("p (c b a) -> p c a b", c=C, a=2, b=2),
         )
 
         w_sb = const.tile([P, 4, F], BF16, name="w_sb")
-        for ob in range(4):
-            nc.sync.dma_start(out=w_sb[:, ob, :], in_=W[ob * P : (ob + 1) * P, :])
         xf = x.rearrange("n c h w -> n c (h w)")
         xbs = []
         xbos = []
@@ -63,16 +65,22 @@ def tile_fast2order_de_conv_t_kernel(tc, x, W, out):
             nc.gpsimd.dma_start(
                 out=xa_part[g0:P:4, :, 0:914], in_=xf[:, :, a0 : a0 + 914].rearrange("n c q -> c n q")
             )
-
-        def load_image(queue, n):
-            xb = xpool.tile([P, LEN], BF16, name="xb")
-            xbs.append(xb)
+        def load_columns(queue, n, c0, c1):
+            xb = const.tile([P, c1 - c0], BF16, name="xb%d_%d" % (n, c0))
             for g0 in range(4):
-                j1 = g0 % 2
-                queue.dma_start(out=xb[g0:P:4, :], in_=xf[n, :, SIDE * j1 : SIDE * j1 + LEN])
+                u0 = SIDE * (g0 % 2)
+                queue.dma_start(out=xb[g0:P:4, :], in_=xf[n, :, u0 + c0 : u0 + c1])
+            return (xb, c0)
 
+        first_tile = load_columns(nc.sync, 0, 0, FIRST)
+        nc.sync.dma_start(out=w_sb[:], in_=W.rearrange("(o j) f -> o j f", j=4))
         for n in range(B):
-            load_image(nc.sync if n <= SYNC_IMAGES else nc.gpsimd, n)
+            queue = nc.sync if n <= SYNC_IMAGES else nc.gpsimd
+            xbs.append(load_columns(queue, n, 0 if n else REST, LEN))
+
+        def columns(n, c0, c1):
+            tile, base = first_tile if n == 0 and c1 <= FIRST else xbs[n]
+            return tile[:, c0 - base : c1 - base]
 
         gs = []
         for k in range(NG):
@@ -92,31 +100,35 @@ def tile_fast2order_de_conv_t_kernel(tc, x, W, out):
         wg = const.tile([P, O, 4], BF16, name="wg", align_bytes=64)
         w_codes = const.tile([P, O], U32, name="w_codes", align_bytes=64)
         w_scales = const.tile([P, O], U8, name="w_scales", align_bytes=64)
-        for ob in range(4):
-            wv = w_sb[:, ob, :].rearrange(
-                "o (ci i0 j1 j0) -> o i0 j0 ci j1", i0=2, j1=2, j0=2
-            )
-            for i0 in range(2):
-                copy = nc.vector.tensor_copy if i0 == 0 else nc.scalar.copy
-                copy(
-                    out=w_perm[:, ob, 2 * i0 : 2 * i0 + 2, :].rearrange(
-                        "o j0 (ci j1) -> o j0 ci j1", j1=2
-                    ),
-                    in_=wv[:, i0],
+        def permute_weights():
+            for ob in range(4):
+                wv = w_sb[:, ob, :].rearrange(
+                    "o (ci i0 j1 j0) -> o i0 j0 ci j1", i0=2, j1=2, j0=2
                 )
+                for i0 in range(2):
+                    copy = nc.vector.tensor_copy if i0 == 0 else nc.scalar.copy
+                    copy(
+                        out=w_perm[:, ob, 2 * i0 : 2 * i0 + 2, :].rearrange(
+                            "o j0 (ci j1) -> o j0 ci j1", j1=2
+                        ),
+                        in_=wv[:, i0],
+                    )
+
+        def transpose_weights(ob):
             xt = psum.tile([P, 4, P], BF16, name="xt", tag="bank")
             for t in range(4):
                 nc.tensor.transpose(xt[:, t, :], w_perm[:, ob, t, :], ident[:])
+            nc.scalar.copy(out=wg[:, ob * P : (ob + 1) * P, :], in_=xt[:].rearrange("p t o -> p o t"))
+
+        def quantise_weights(ob):
             cols = slice(ob * P, (ob + 1) * P)
-            copy = nc.vector.tensor_copy if ob % 2 == 0 else nc.scalar.copy
-            copy(out=wg[:, cols, :], in_=xt[:].rearrange("p t o -> p o t"))
             nc.vector.quantize_mx(
                 out=w_codes[:, cols].bitcast(FP8X4),
                 scales=w_scales[:, cols],
                 in_=wg[:, cols, :].rearrange("p o t -> p (o t)"),
             )
 
-        out_v = out.rearrange("n (mt o) y z -> n mt o (y z)", o=P)
+        out_v = out.rearrange("n (o mt) y z -> n mt o (y z)", mt=4)
 
         plan = []
         nfull = 0
@@ -137,25 +149,29 @@ def tile_fast2order_de_conv_t_kernel(tc, x, W, out):
                     nfull += 1
 
         def piece_ends(n, w, mt):
-            if w == 7 and n == B - 1:
+            if n == 0 and w == 0:
                 return True
-            return w == 9 or (w < 8 and (w - mt) % PERIOD == PERIOD - 1)
+            short = (n == 0 and w < 4) or (n == B - 1 and w > 3)
+            period = 2 if short else PERIOD
+            return w == 9 or (w < 8 and (w - mt) % period == period - 1)
 
         def piece_starts(n, w, mt):
             return w == 0 or piece_ends(n, w - 1, mt)
 
         state = {}
+        deferred = []
         late = []
 
         def emit_shifted(win):
-            piece = None if win["small"] else XBO_PIECES.get(win["y0"] // WROWS)
+            pieces = XBO_PIECES if win["n"] else XBO_PIECES_0
+            piece = None if win["small"] else pieces.get(win["y0"] // WROWS)
             if piece is not None:
                 if piece[0] == 0:
                     xbo = opool.tile([P, LEN], BF16, name="xbo")
                     xbos.append(xbo)
                 nc.vector.tensor_copy(
                     out=xbos[win["n"]][:, piece[0] : piece[1]],
-                    in_=xbs[win["n"]][:, piece[0] + 1 : piece[1] + 1],
+                    in_=columns(win["n"], piece[0] + 1, piece[1] + 1),
                 )
             if not win["pe"]:
                 local = SIDE * (win["y0"] - WROWS * PLAIN_WINDOWS[0])
@@ -164,31 +180,37 @@ def tile_fast2order_de_conv_t_kernel(tc, x, W, out):
                     in_=xa_part[:, win["n"], local : local + 458].unsqueeze(2).to_broadcast([P, 458, 2]),
                 )
 
-        def emit_products(win):
+        def emit_doubled(win):
             n = win["n"]
             q0 = SIDE * win["y0"]
             small = win["small"]
             m = 32 if small else HALF
-            gt = gsmall[win["slot"]] if small else gs[win["slot"]]
-            xad_flat = None
             if win["pe"]:
                 xad = psum_x.tile([P, 2 * SLOT, 2], BF16, name="xad")
                 for r0, r1 in ((0, 2 * m + 1),) if small else ((0, SLOT), (SLOT, 2 * m + 1)):
                     nc.tensor.matmul(
                         out=xad[:, r0:r1, :],
                         lhsT=swap[:],
-                        rhs=xbs[n][:, q0 + r0 : q0 + r1].unsqueeze(2).to_broadcast([P, r1 - r0, 2]),
+                        rhs=columns(n, q0 + r0, q0 + r1).unsqueeze(2).to_broadcast([P, r1 - r0, 2]),
                         start=True,
                         stop=True,
                     )
-                xad_flat = xad[:].rearrange("p r e -> p (r e)")
+                win["xad"] = xad[:].rearrange("p r e -> p (r e)")
             else:
-                xad_flat = xa2s[(win["y0"] // WROWS) % 2][:].rearrange("p r e -> p (r e)")
+                win["xad"] = xa2s[(win["y0"] // WROWS) % 2][:].rearrange("p r e -> p (r e)")
+
+        def emit_products(win):
+            n = win["n"]
+            q0 = SIDE * win["y0"]
+            small = win["small"]
+            m = 32 if small else HALF
+            gt = gsmall[win["slot"]] if small else gs[win["slot"]]
+            xad_flat = win["xad"]
             for s in range(2):
                 in0 = xad_flat[:, 2 * s : 2 * s + 4 * m].rearrange("p (m i j) -> p m i j", i=2, j=2)
                 start = q0 + s
                 if start % 2 == 0:
-                    pairs = xbs[n][:, start : start + 2 * m]
+                    pairs = columns(n, start, start + 2 * m)
                 else:
                     pairs = xbos[n][:, start - 1 : start - 1 + 2 * m]
                 in1 = (
@@ -226,10 +248,11 @@ def tile_fast2order_de_conv_t_kernel(tc, x, W, out):
                 in_=ps[:, :, 195:227].rearrange("p s a -> p a s"),
             )
 
-        def emit_rest(win):
-            small = win["small"]
-            width = GRID if small else 2 * SLOT
-            if small:
+        def store(n, mt, st, pos0, size):
+            nc.sync.dma_start(out=out_v[n, mt][:, pos0 : pos0 + size], in_=st[:, 0:size])
+
+        def emit_quantise(win):
+            if win["small"]:
                 g_flat = gsmall[win["slot"]][:].rearrange("p m t -> p (m t)")
                 codes = cpool.tile([P, GRID], U32, name="codes_s", align_bytes=64)
                 scales = cpool.tile([P, GRID], U8, name="scales_s", align_bytes=64)
@@ -238,10 +261,16 @@ def tile_fast2order_de_conv_t_kernel(tc, x, W, out):
                 codes = cpool.tile([P, 2 * SLOT], U32, name="codes", align_bytes=64)
                 scales = cpool.tile([P, 2 * SLOT], U8, name="scales", align_bytes=64)
             nc.vector.quantize_mx(out=codes[:].bitcast(FP8X4), scales=scales[:], in_=g_flat)
+            win["moving"] = (codes, scales)
+
+        def emit_matmuls(win):
+            small = win["small"]
+            width = GRID if small else 2 * SLOT
+            codes, scales = win["moving"]
             w = win["w"]
             for mt in range(4):
                 if piece_starts(win["n"], w, mt):
-                    st = stage.tile([P, STAGE], F32, name="st")
+                    st = stage.tile([P, STAGE], F32, name="st", align_bytes=256)
                     state[mt] = (st, win["y0"])
                 st, row_first = state[mt]
                 b0 = (win["y0"] - row_first) * GRID
@@ -255,27 +284,50 @@ def tile_fast2order_de_conv_t_kernel(tc, x, W, out):
                     start=True,
                     stop=True,
                 )
+                help_here = win["n"] == B - 1 and w >= HELP_FROM and mt % 2 == 1
                 if (w, mt) in LEND and win["n"] < B - 1:
-                    late.append([2, ps, st, b0])
+                    late.append([3, ps, st, b0])
+                elif help_here:
+                    deferred.append((evacuate, (nc.vector.tensor_copy, ps, st, b0, small)))
                 else:
                     evacuate(nc.scalar.copy, ps, st, b0, small)
                 if piece_ends(win["n"], w, mt):
                     size = b0 + (GRID if small else WROWS * GRID)
-                    pos0 = row_first * GRID
-                    nc.sync.dma_start(out=out_v[win["n"], mt][:, pos0 : pos0 + size], in_=st[:, 0:size])
+                    piece = (win["n"], mt, st, row_first * GRID, size)
+                    if help_here:
+                        deferred.append((store, piece))
+                    else:
+                        store(*piece)
 
-        prev = None
         emit_shifted(plan[0])
+        emit_doubled(plan[0])
+        emit_doubled(plan[1])
+        permute_weights()
+        emit_products(plan[0])
+        for ob in range(4):
+            transpose_weights(ob)
         emit_shifted(plan[1])
-        for k, win in enumerate(plan):
+        emit_products(plan[1])
+        emit_doubled(plan[2])
+        quantise_weights(0)
+        emit_quantise(plan[0])
+        for ob in range(1, 4):
+            quantise_weights(ob)
+        emit_shifted(plan[2])
+
+        for k in range(len(plan)):
+            if k + 3 < len(plan):
+                emit_doubled(plan[k + 3])
             if k + 2 < len(plan):
-                emit_shifted(plan[k + 2])
-            emit_products(win)
-            if prev is not None:
-                emit_rest(prev)
-            prev = win
+                emit_products(plan[k + 2])
+            if k + 1 < len(plan):
+                emit_quantise(plan[k + 1])
+            emit_matmuls(plan[k])
             for item in late:
                 item[0] -= 1
                 if item[0] == 0:
                     evacuate(nc.vector.tensor_copy, item[1], item[2], item[3], False)
-        emit_rest(prev)
+            if k + 3 < len(plan):
+                emit_shifted(plan[k + 3])
+        for call, args in deferred:
+            call(*args)

@@ -22,7 +22,7 @@ SLOT = 256
 WROWS = 7
 HALF = 228
 NG = 4
-PLAIN_WINDOWS = (4, 5)
+PLAIN_WINDOWS = (5, 6)
 XBO_PIECES = {0: (0, 1820), 4: (1820, 2730), 6: (2730, 4158)}
 XBO_PIECES_0 = {0: (0, 456), 1: (456, 1366), 3: (1366, 1820), 4: (1820, 2730), 6: (2730, 4158)}
 FIRST = 1376
@@ -30,7 +30,7 @@ REST = 1364
 SYNC_IMAGES = 2
 XAW = 928
 PERIOD = 4
-HELP_FROM = 6
+HELP_FROM = 8
 STAGE = (PERIOD * WROWS + 1) * GRID
 LEND = ((6, 2),)
 FLOPS = 2 * O * F * B * GRID * GRID
@@ -44,8 +44,8 @@ def tile_fast2order_de_conv_t_kernel(tc, x, W, out):
         opool = ctx.enter_context(tc.tile_pool(name="opool", bufs=2))
         cpool = ctx.enter_context(tc.tile_pool(name="cpool", bufs=4))
         stage = ctx.enter_context(tc.tile_pool(name="stage", bufs=18))
-        psum = ctx.enter_context(tc.psum_pool(name="psum", bufs=6))
-        psum_x = ctx.enter_context(tc.psum_pool(name="psum_x", bufs=2))
+        psum = ctx.enter_context(tc.psum_pool(name="psum", bufs=5))
+        psum_x = ctx.enter_context(tc.psum_pool(name="psum_x", bufs=3))
 
         ident = const.tile([P, P], BF16, name="ident")
         make_identity(nc, ident[:])
@@ -173,6 +173,8 @@ def tile_fast2order_de_conv_t_kernel(tc, x, W, out):
                     out=xbos[win["n"]][:, piece[0] : piece[1]],
                     in_=columns(win["n"], piece[0] + 1, piece[1] + 1),
                 )
+
+        def emit_plain(win):
             if not win["pe"]:
                 local = SIDE * (win["y0"] - WROWS * PLAIN_WINDOWS[0])
                 nc.vector.tensor_copy(
@@ -300,34 +302,39 @@ def tile_fast2order_de_conv_t_kernel(tc, x, W, out):
                         store(*piece)
 
         emit_shifted(plan[0])
-        emit_doubled(plan[0])
-        emit_doubled(plan[1])
+        for k in range(3):
+            emit_doubled(plan[k])
         permute_weights()
         emit_products(plan[0])
         for ob in range(4):
             transpose_weights(ob)
         emit_shifted(plan[1])
         emit_products(plan[1])
-        emit_doubled(plan[2])
+        emit_doubled(plan[3])
         quantise_weights(0)
         emit_quantise(plan[0])
         for ob in range(1, 4):
             quantise_weights(ob)
         emit_shifted(plan[2])
+        emit_products(plan[2])
+        emit_quantise(plan[1])
+        emit_shifted(plan[3])
 
         for k in range(len(plan)):
+            if k + 4 < len(plan):
+                emit_doubled(plan[k + 4])
             if k + 3 < len(plan):
-                emit_doubled(plan[k + 3])
+                emit_products(plan[k + 3])
+            if k + 4 < len(plan):
+                emit_plain(plan[k + 4])
             if k + 2 < len(plan):
-                emit_products(plan[k + 2])
-            if k + 1 < len(plan):
-                emit_quantise(plan[k + 1])
+                emit_quantise(plan[k + 2])
             emit_matmuls(plan[k])
             for item in late:
                 item[0] -= 1
                 if item[0] == 0:
                     evacuate(nc.vector.tensor_copy, item[1], item[2], item[3], False)
-            if k + 3 < len(plan):
-                emit_shifted(plan[k + 3])
+            if k + 4 < len(plan):
+                emit_shifted(plan[k + 4])
         for call, args in deferred:
             call(*args)

@@ -24,15 +24,15 @@ HALF = 228
 NG = 4
 PLAIN_WINDOWS = (5, 6)
 XBO_PIECES = {0: (0, 1820), 4: (1820, 2730), 6: (2730, 4158)}
-XBO_PIECES_0 = {0: (0, 456), 1: (456, 1366), 3: (1366, 1820), 4: (1820, 2730), 6: (2730, 4158)}
-FIRST = 1376
-REST = 1364
+XBO_PIECES_0 = {0: (0, 456), 1: (456, 910), 2: (910, 1820), 4: (1820, 2730), 6: (2730, 4158)}
+FIRST = 912
+REST = 910
 SYNC_IMAGES = 2
 XAW = 928
-PERIOD = 4
+PERIOD = 3
 HELP_FROM = 8
 STAGE = (PERIOD * WROWS + 1) * GRID
-LEND = ((6, 2),)
+LEND = ((6, 3),)
 FLOPS = 2 * O * F * B * GRID * GRID
 
 
@@ -43,7 +43,7 @@ def tile_fast2order_de_conv_t_kernel(tc, x, W, out):
         const = ctx.enter_context(tc.tile_pool(name="const", bufs=1))
         opool = ctx.enter_context(tc.tile_pool(name="opool", bufs=2))
         cpool = ctx.enter_context(tc.tile_pool(name="cpool", bufs=4))
-        stage = ctx.enter_context(tc.tile_pool(name="stage", bufs=18))
+        stage = ctx.enter_context(tc.tile_pool(name="stage", bufs=24))
         psum = ctx.enter_context(tc.psum_pool(name="psum", bufs=5))
         psum_x = ctx.enter_context(tc.psum_pool(name="psum_x", bufs=3))
 
@@ -149,11 +149,9 @@ def tile_fast2order_de_conv_t_kernel(tc, x, W, out):
                     nfull += 1
 
         def piece_ends(n, w, mt):
-            if n == 0 and w == 0:
+            if n == B - 1 and w == 7 and mt != 1:
                 return True
-            short = (n == 0 and w < 4) or (n == B - 1 and w > 3)
-            period = 2 if short else PERIOD
-            return w == 9 or (w < 8 and (w - mt) % period == period - 1)
+            return w == 9 or (w < 8 and (w - mt) % PERIOD == PERIOD - 1)
 
         def piece_starts(n, w, mt):
             return w == 0 or piece_ends(n, w - 1, mt)
@@ -302,12 +300,13 @@ def tile_fast2order_de_conv_t_kernel(tc, x, W, out):
                         store(*piece)
 
         emit_shifted(plan[0])
-        for k in range(3):
+        for k in range(2):
             emit_doubled(plan[k])
         permute_weights()
         emit_products(plan[0])
         for ob in range(4):
             transpose_weights(ob)
+        emit_doubled(plan[2])
         emit_shifted(plan[1])
         emit_products(plan[1])
         emit_doubled(plan[3])

from contextlib import ExitStack

import concourse.mybir as mybir
from concourse.masks import make_identity

BF16 = mybir.dt.bfloat16
F32 = mybir.dt.float32
U32 = mybir.dt.uint32
U8 = mybir.dt.uint8
FP8X4 = mybir.dt.float8_e4m3fn_x4
MULT = mybir.AluOpType.mult

P = 128
B = 4
C = 32
SIDE = 65
GRID = 64
O = 512
F = 512
LEN = GRID * SIDE
SLOT = 256
WROWS = 7
HALF = 228
NG = 4
PLAIN_WINDOWS = (5, 6)
XBO_PIECES = {0: (0, 1820), 4: (1820, 2730), 6: (2730, 4158)}
XBO_PIECES_0 = {0: (0, 456), 1: (456, 910), 2: (910, 1820), 4: (1820, 2730), 6: (2730, 4158)}
FIRST = 912
REST = 910
SYNC_IMAGES = 2
XAW = 928
PERIOD = 3
HELP_FROM = 8
STAGE = (PERIOD * WROWS + 1) * GRID
LEND = ((6, 3),)
FLOPS = 2 * O * F * B * GRID * GRID


def tile_fast2order_de_conv_t_kernel(tc, x, W, out):
    nc = tc.nc
    with ExitStack() as ctx:
        ctx.enter_context(tc.manual_schedule())
        const = ctx.enter_context(tc.tile_pool(name="const", bufs=1))
        opool = ctx.enter_context(tc.tile_pool(name="opool", bufs=2))
        cpool = ctx.enter_context(tc.tile_pool(name="cpool", bufs=4))
        stage = ctx.enter_context(tc.tile_pool(name="stage", bufs=24))
        psum = ctx.enter_context(tc.psum_pool(name="psum", bufs=5))
        psum_x = ctx.enter_context(tc.psum_pool(name="psum_x", bufs=3))

        ident = const.tile([P, P], BF16, name="ident")
        make_identity(nc, ident[:])
        swap = const.tile([P, P], BF16, name="swap")
        nc.gpsimd.tensor_copy(
            out=swap[:].rearrange("p (c a b) -> p c a b", c=C, a=2, b=2),
            in_=ident[:].rearrange("p (c b a) -> p c a b", c=C, a=2, b=2),
        )

        w_sb = const.tile([P, 4, F], BF16, name="w_sb")
        xf = x.rearrange("n c h w -> n c (h w)")
        xbs = []
        xbos = []
        xa_part = const.tile([P, B, XAW], BF16, name="xa_part")
        for g0 in range(4):
            a0 = SIDE * (WROWS * PLAIN_WINDOWS[0] + g0 // 2)
            nc.gpsimd.dma_start(
                out=xa_part[g0:P:4, :, 0:914], in_=xf[:, :, a0 : a0 + 914].rearrange("n c q -> c n q")
            )
        def load_columns(queue, n, c0, c1):
            xb = const.tile([P, c1 - c0], BF16, name="xb%d_%d" % (n, c0))
            for g0 in range(4):
                u0 = SIDE * (g0 % 2)
                queue.dma_start(out=xb[g0:P:4, :], in_=xf[n, :, u0 + c0 : u0 + c1])
            return (xb, c0)

        first_tile = load_columns(nc.sync, 0, 0, FIRST)
        nc.sync.dma_start(out=w_sb[:], in_=W.rearrange("(o j) f -> o j f", j=4))
        for n in range(B):
            queue = nc.sync if n <= SYNC_IMAGES else nc.gpsimd
            xbs.append(load_columns(queue, n, 0 if n else REST, LEN))

        def columns(n, c0, c1):
            tile, base = first_tile if n == 0 and c1 <= FIRST else xbs[n]
            return tile[:, c0 - base : c1 - base]

        gs = []
        for k in range(NG):
            gt = const.tile([P, 2, SLOT, 4], BF16, name="g%d" % k, align_bytes=64)
            nc.vector.memset(gt[:, :, HALF:SLOT, :], 0.0)
            gs.append(gt)
        xa2s = []
        for k in range(2):
            xa2 = const.tile([P, 458, 2], BF16, name="xa2_%d" % k)
            xa2s.append(xa2)
        gsmall = []
        for k in range(2):
            gt = const.tile([P, GRID, 4], BF16, name="gsmall%d" % k, align_bytes=64)
            gsmall.append(gt)

        w_perm = const.tile([P, 4, 4, P], BF16, name="w_perm")
        wg = const.tile([P, O, 4], BF16, name="wg", align_bytes=64)
        w_codes = const.tile([P, O], U32, name="w_codes", align_bytes=64)
        w_scales = const.tile([P, O], U8, name="w_scales", align_bytes=64)
        def permute_weights():
            for ob in range(4):
                wv = w_sb[:, ob, :].rearrange(
                    "o (ci i0 j1 j0) -> o i0 j0 ci j1", i0=2, j1=2, j0=2
                )
                for i0 in range(2):
                    copy = nc.vector.tensor_copy if i0 == 0 else nc.scalar.copy
                    copy(
                        out=w_perm[:, ob, 2 * i0 : 2 * i0 + 2, :].rearrange(
                            "o j0 (ci j1) -> o j0 ci j1", j1=2
                        ),
                        in_=wv[:, i0],
                    )

        def transpose_weights(ob):
            xt = psum.tile([P, 4, P], BF16, name="xt", tag="bank")
            for t in range(4):
                nc.tensor.transpose(xt[:, t, :], w_perm[:, ob, t, :], ident[:])
            nc.scalar.copy(out=wg[:, ob * P : (ob + 1) * P, :], in_=xt[:].rearrange("p t o -> p o t"))

        def quantise_weights(ob):
            cols = slice(ob * P, (ob + 1) * P)
            nc.vector.quantize_mx(
                out=w_codes[:, cols].bitcast(FP8X4),
                scales=w_scales[:, cols],
                in_=wg[:, cols, :].rearrange("p o t -> p (o t)"),
            )

        out_v = out.rearrange("n (o mt) y z -> n mt o (y z)", mt=4)

        plan = []
        nfull = 0
        for n in range(B):
            for w in range(10):
                small = w == 9
                plan.append(
                    {
                        "n": n,
                        "w": w,
                        "y0": WROWS * w,
                        "small": small,
                        "pe": small or w not in PLAIN_WINDOWS,
                        "slot": n % 2 if small else nfull % NG,
                    }
                )
                if not small:
                    nfull += 1

        def piece_ends(n, w, mt):
            if n == B - 1 and w == 7 and mt != 1:
                return True
            return w == 9 or (w < 8 and (w - mt) % PERIOD == PERIOD - 1)

        def piece_starts(n, w, mt):
            return w == 0 or piece_ends(n, w - 1, mt)

        state = {}
        deferred = []
        late = []

        def emit_shifted(win):
            pieces = XBO_PIECES if win["n"] else XBO_PIECES_0
            piece = None if win["small"] else pieces.get(win["y0"] // WROWS)
            if piece is not None:
                if piece[0] == 0:
                    xbo = opool.tile([P, LEN], BF16, name="xbo")
                    xbos.append(xbo)
                nc.vector.tensor_copy(
                    out=xbos[win["n"]][:, piece[0] : piece[1]],
                    in_=columns(win["n"], piece[0] + 1, piece[1] + 1),
                )

        def emit_plain(win):
            if not win["pe"]:
                local = SIDE * (win["y0"] - WROWS * PLAIN_WINDOWS[0])
                nc.vector.tensor_copy(
                    out=xa2s[(win["y0"] // WROWS) % 2][:],
                    in_=xa_part[:, win["n"], local : local + 458].unsqueeze(2).to_broadcast([P, 458, 2]),
                )

        def emit_doubled(win):
            n = win["n"]
            q0 = SIDE * win["y0"]
            small = win["small"]
            m = 32 if small else HALF
            if win["pe"]:
                xad = psum_x.tile([P, 2 * SLOT, 2], BF16, name="xad")
                for r0, r1 in ((0, 2 * m + 1),) if small else ((0, SLOT), (SLOT, 2 * m + 1)):
                    nc.tensor.matmul(
                        out=xad[:, r0:r1, :],
                        lhsT=swap[:],
                        rhs=columns(n, q0 + r0, q0 + r1).unsqueeze(2).to_broadcast([P, r1 - r0, 2]),
                        start=True,
                        stop=True,
                    )
                win["xad"] = xad[:].rearrange("p r e -> p (r e)")
            else:
                win["xad"] = xa2s[(win["y0"] // WROWS) % 2][:].rearrange("p r e -> p (r e)")

        def emit_products(win):
            n = win["n"]
            q0 = SIDE * win["y0"]
            small = win["small"]
            m = 32 if small else HALF
            gt = gsmall[win["slot"]] if small else gs[win["slot"]]
            xad_flat = win["xad"]
            for s in range(2):
                in0 = xad_flat[:, 2 * s : 2 * s + 4 * m].rearrange("p (m i j) -> p m i j", i=2, j=2)
                start = q0 + s
                if start % 2 == 0:
                    pairs = columns(n, start, start + 2 * m)
                else:
                    pairs = xbos[n][:, start - 1 : start - 1 + 2 * m]
                in1 = (
                    pairs.rearrange("p (m j) -> p m j", j=2).unsqueeze(2).to_broadcast([P, m, 2, 2])
                )
                dst = gt[:, s * m : (s + 1) * m, :] if small else gt[:, s, 0:m, :]
                nc.vector.tensor_tensor(
                    out=dst.rearrange("p m (i j) -> p m i j", i=2), in0=in0, in1=in1, op=MULT
                )

        def evacuate(copy, ps, st, b0, small):
            if small:
                copy(
                    out=st[:, b0 : b0 + GRID].rearrange("p (a s) -> p a s", s=2),
                    in_=ps[:].rearrange("p s a -> p a s"),
                )
                return
            copy(
                out=st[:, b0 + 64 : b0 + 64 + 384]
                .rearrange("p (rho e) -> p rho e", e=128)[:, :, 0:64]
                .rearrange("p rho (k s) -> p rho k s", s=2),
                in_=ps[:]
                .rearrange("p s k -> p (s k)")[:, 0:510]
                .rearrange("p (e x) -> p e x", x=255)[:, ::-1, 33:228]
                .rearrange("p e (rho k) -> p rho k e", k=65)[:, :, 0:32, :],
            )
            copy(
                out=st[:, b0 : b0 + 384]
                .rearrange("p (rho e) -> p rho e", e=128)[:, :, 0:64]
                .rearrange("p rho (a s) -> p rho a s", s=2),
                in_=ps[:, :, 0:195].rearrange("p s (rho k) -> p rho k s", k=65)[:, :, 0:32, :],
            )
            copy(
                out=st[:, b0 + 384 : b0 + 448].rearrange("p (a s) -> p a s", s=2),
                in_=ps[:, :, 195:227].rearrange("p s a -> p a s"),
            )

        def store(n, mt, st, pos0, size):
            nc.sync.dma_start(out=out_v[n, mt][:, pos0 : pos0 + size], in_=st[:, 0:size])

        def emit_quantise(win):
            if win["small"]:
                g_flat = gsmall[win["slot"]][:].rearrange("p m t -> p (m t)")
                codes = cpool.tile([P, GRID], U32, name="codes_s", align_bytes=64)
                scales = cpool.tile([P, GRID], U8, name="scales_s", align_bytes=64)
            else:
                g_flat = gs[win["slot"]][:].rearrange("p s m t -> p (s m t)")
                codes = cpool.tile([P, 2 * SLOT], U32, name="codes", align_bytes=64)
                scales = cpool.tile([P, 2 * SLOT], U8, name="scales", align_bytes=64)
            nc.vector.quantize_mx(out=codes[:].bitcast(FP8X4), scales=scales[:], in_=g_flat)
            win["moving"] = (codes, scales)

        def emit_matmuls(win):
            small = win["small"]
            width = GRID if small else 2 * SLOT
            codes, scales = win["moving"]
            w = win["w"]
            for mt in range(4):
                if piece_starts(win["n"], w, mt):
                    st = stage.tile([P, STAGE], F32, name="st", align_bytes=256)
                    state[mt] = (st, win["y0"])
                st, row_first = state[mt]
                b0 = (win["y0"] - row_first) * GRID
                ps = psum.tile([P, 2, width // 2], F32, name="ps", tag="bank")
                nc.tensor.matmul_mx(
                    out=ps[:].rearrange("p s k -> p (s k)"),
                    lhsT=w_codes[:, mt * P : (mt + 1) * P].bitcast(FP8X4),
                    lhsT_scale=w_scales[:, mt * P : (mt + 1) * P],
                    rhs=codes[:].bitcast(FP8X4),
                    rhs_scale=scales[:],
                    start=True,
                    stop=True,
                )
                help_here = win["n"] == B - 1 and w >= HELP_FROM and mt % 2 == 1
                if (w, mt) in LEND and win["n"] < B - 1:
                    late.append([3, ps, st, b0])
                elif help_here:
                    deferred.append((evacuate, (nc.vector.tensor_copy, ps, st, b0, small)))
                else:
                    evacuate(nc.scalar.copy, ps, st, b0, small)
                if piece_ends(win["n"], w, mt):
                    size = b0 + (GRID if small else WROWS * GRID)
                    piece = (win["n"], mt, st, row_first * GRID, size)
                    if help_here:
                        deferred.append((store, piece))
                    else:
                        store(*piece)

        emit_shifted(plan[0])
        for k in range(2):
            emit_doubled(plan[k])
        permute_weights()
        emit_products(plan[0])
        for ob in range(4):
            transpose_weights(ob)
        emit_doubled(plan[2])
        emit_shifted(plan[1])
        emit_products(plan[1])
        emit_doubled(plan[3])
        quantise_weights(0)
        emit_quantise(plan[0])
        for ob in range(1, 4):
            quantise_weights(ob)
        emit_shifted(plan[2])
        emit_products(plan[2])
        emit_quantise(plan[1])
        emit_shifted(plan[3])

        for k in range(len(plan)):
            if k + 4 < len(plan):
                emit_doubled(plan[k + 4])
            if k + 3 < len(plan):
                emit_products(plan[k + 3])
            if k + 4 < len(plan):
                emit_plain(plan[k + 4])
            if k + 2 < len(plan):
                emit_quantise(plan[k + 2])
            emit_matmuls(plan[k])
            for item in late:
                item[0] -= 1
                if item[0] == 0:
                    evacuate(nc.vector.tensor_copy, item[1], item[2], item[3], False)
            if k + 4 < len(plan):
                emit_shifted(plan[k + 4])
        for call, args in deferred:
            call(*args)
